import numpy as np
import ml_dtypes


def mxq(x, axis, fmt="e4m3"):
    dtype, down = {"e4m3": (ml_dtypes.float8_e4m3fn, 7), "e5m2": (ml_dtypes.float8_e5m2, 14)}[fmt]
    v = np.moveaxis(np.asarray(x, np.float32).astype(ml_dtypes.bfloat16).astype(np.float64), axis, -1)
    blocks = v.reshape(v.shape[:-1] + (-1, 32))
    amax = np.abs(blocks).max(-1, keepdims=True)
    byte = np.maximum(np.where(amax > 0, np.frexp(amax)[1] - 1 + 127, 0) - down, 1)
    scale = np.exp2(byte - 127.0)
    codes = (blocks / scale).astype(np.float32).astype(dtype).astype(np.float64)
    return np.moveaxis((codes * scale).reshape(v.shape), -1, axis)


WIDE = False


def mx_kscale(k):
    if not WIDE:
        return np.ones(k)
    levels = np.array([30, -30])
    if k % 512:
        return np.exp2(np.random.permutation(np.resize(levels, k // 32))).repeat(32)
    a = np.empty((k // 512, 16))
    for p in range(k // 512):
        a[p, :8] = np.random.permutation(np.resize(levels, 8))
        for g in range(8):
            far = levels[np.abs(levels - a[p, g]) >= 10]
            a[p, g + 8] = far[np.random.randint(len(far))]
    return np.exp2(a.ravel()).repeat(32)


BF16 = ml_dtypes.bfloat16


def bf(x):
    return np.asarray(x, np.float32).astype(BF16)


def f64(x):
    return np.asarray(x).astype(np.float64)


E2M1 = np.array([0.0, 0.5, 1.0, 1.5, 2.0, 3.0, 4.0, 6.0, -0.0, -0.5, -1.0, -1.5, -2.0, -3.0, -4.0, -6.0])


def pack_weight(w, fmt):
    k, n = w.shape
    w = f64(bf(w)).reshape(k // 32, 32, n)
    amax = np.abs(w).max(1)
    if fmt == "e4m3":
        byte = np.frexp(amax)[1] - 1 + 127 - 7
    else:
        mant, ex = np.frexp(amax / 6.0)
        byte = np.where(mant > 0.5, ex, ex - 1) + 127
    byte = np.clip(np.where(amax > 0, byte, 1), 1, 254)
    scaled = (w * np.exp2(127.0 - byte)[:, None, :]).reshape(k, n).astype(np.float32)
    by_word = np.ascontiguousarray(scaled.reshape(k // 512, 128, 4, n).transpose(0, 1, 3, 2))
    if fmt == "e4m3":
        words = by_word.astype(ml_dtypes.float8_e4m3fn).view(np.uint8)
    else:
        c = by_word.astype(ml_dtypes.float4_e2m1fn).view(np.uint8) & 0xF
        words = c[..., 0::2] | (c[..., 1::2] << 4)
    return np.ascontiguousarray(words), np.ascontiguousarray(byte.astype(np.uint8).reshape(k // 512, 16, n))


def unpack_weight(words, scales, fmt):
    g, p, n, _ = words.shape
    if fmt == "e4m3":
        vals = np.ascontiguousarray(words).view(ml_dtypes.float8_e4m3fn).astype(np.float64)
    else:
        nib = np.empty((g, p, n, 4), np.uint8)
        nib[..., 0::2] = words & 0xF
        nib[..., 1::2] = words >> 4
        vals = E2M1[nib]
    vals = vals * np.repeat(np.exp2(scales.astype(np.float64) - 127.0), 8, axis=1)[..., None]
    return vals.transpose(0, 1, 3, 2).reshape(g * 512, n)

def pack4(w):
    words, scales = pack_weight(w, "e2m1")
    return words.reshape(words.shape[0], 128, -1), scales


def unpack4(words, scales):
    return unpack_weight(words.reshape(words.shape[0], 128, -1, 2), scales, "e2m1")


B, DI, DH = 1024, 1024, 256


def sigmoid(v):
    return 1.0 / (1.0 + np.exp(-v))


def setup_inputs():
    s = mx_kscale(DI)
    n = np.random.standard_normal
    a, c = 0.7 / np.sqrt(DI), 0.7 / np.sqrt(DH)
    keep = np.random.uniform(size=B) < 0.9
    out = {
        "x": bf(n((B, DI)) * s),
        "h_minors": bf(n((B, DH))),
        "c_minors": bf(n((B, DH))),
        "s0": bf(n((B, DH))),
        "s1": bf(n((B, DH))),
        "s2": bf(n((B, DH))),
        "mask": bf(keep * (0.5 + 0.5 * np.random.uniform(size=B))),
    }
    words, scales = pack4((n((7 * DH, DI)) * a / s).T)
    out["weight_ih_words"] = words
    out["weight_ih_scales"] = scales
    out.update({
        "bias_ih": bf(n(7 * DH) * 0.3),
        "weight_hh": bf(n((4 * DH, DH)) * c),
        "bias_hh": bf(n(4 * DH) * 0.3),
        "weight_sh0": bf(n((DH, DH)) * c),
        "bias_sh0": bf(n(DH) * 0.3),
        "weight_sh1": bf(n((DH, DH)) * c),
        "bias_sh1": bf(n(DH) * 0.3),
        "weight_sh2": bf(n((DH, DH)) * c),
        "bias_sh2": bf(n(DH) * 0.3),
    })
    return out


def reference(x, h_minors, c_minors, s0, s1, s2, mask, weight_ih_words, weight_ih_scales, bias_ih, weight_hh, bias_hh,
              weight_sh0, bias_sh0, weight_sh1, bias_sh1, weight_sh2, bias_sh2):
    d = DH
    m = f64(mask)[:, None]

    tmp = (mxq(f64(x), 1, "e5m2") @ unpack4(weight_ih_words, weight_ih_scales)) + f64(bias_ih)
    tmp2 = f64(h_minors) @ f64(weight_hh).T + f64(bias_hh)
    tmp3 = np.concatenate([
        f64(s0) @ f64(weight_sh0).T + f64(bias_sh0),
        f64(s1) @ f64(weight_sh1).T + f64(bias_sh1),
        f64(s2) @ f64(weight_sh2).T + f64(bias_sh2),
    ], axis=1)

    tmp_in, tmp_s = tmp[:, :4 * d], tmp[:, 4 * d:]
    pre = tmp_in + tmp2
    ifo = sigmoid(pre[:, :3 * d])
    c_hat = pre[:, 3 * d:]
    i_g, f_g, o_g = ifo[:, :d], ifo[:, d:2 * d], ifo[:, 2 * d:]

    c_t = (f_g * f64(c_minors) + i_g * np.tanh(c_hat)) * m
    tc = np.tanh(c_t) * m
    h = o_g * tc

    bg = sigmoid(tmp_s + tmp3)
    b0, b1, b2 = bg[:, :d], bg[:, d:2 * d], bg[:, 2 * d:]

    s_0 = (b0 + 1.0 - o_g) * tc
    s_1 = (b1 + 2.0 - o_g - s_0) * 0.5 * tc
    s_2 = (b2 + 3.0 - o_g - (2.0 * s_0 + s_1)) * (1.0 / 3.0) * tc

    return (h, c_t, s_0, s_1, s_2)

@@ -1,0 +1,382 @@
+from contextlib import ExitStack
+
+import concourse.mybir as mybir
+from concourse.masks import make_identity
+
+B, DI, DH = 1024, 1024, 256
+NG = 7 * DH
+FLOPS = 2 * B * DI * NG + 2 * B * DH * NG
+
+F32 = mybir.dt.float32
+BF16 = mybir.dt.bfloat16
+I32 = mybir.dt.int32
+U32 = mybir.dt.uint32
+U8 = mybir.dt.uint8
+E5M2X4 = mybir.dt.float8_e5m2_x4
+E2M1X4 = mybir.dt.float4_e2m1fn_x4
+ACT = mybir.ActivationFunctionType
+ALU = mybir.AluOpType
+
+P = 128
+TILES = B // P
+PASSES = DI // 512
+BLOCKS = NG // P
+HH_BLOCKS = 4 * DH // P
+PAIR_ROWS = 2 * P
+HH_PAIRS = [(0, 4), (1, 5), (2, 6), (3, 7)]
+S_PAIRS = [(8, 11), (9, 12), (10, 13)]
+BLOCK_ORDER = [j for pair in HH_PAIRS + S_PAIRS for j in pair]
+OTHER_BIAS_ROW = 16
+PAIR_SLOTS = [(0, 2, 4, 6, 8)] + [(2, 5, 8, 11), (0, 3, 6)] * 3 + [()]
+
+
+def tile_share_lstm_cell_pa_kernel(
+    tc, x, h_minors, c_minors, s0, s1, s2, mask, weight_ih_words, weight_ih_scales, bias_ih,
+    weight_hh, bias_hh, weight_sh0, bias_sh0, weight_sh1, bias_sh1, weight_sh2, bias_sh2,
+    out_0, out_1, out_2, out_3, out_4,
+):
+    nc = tc.nc
+    with ExitStack() as ctx:
+        keep = ctx.enter_context(tc.tile_pool(name="keep", bufs=1))
+        work = ctx.enter_context(tc.tile_pool(name="work", bufs=2))
+        psum = ctx.enter_context(tc.psum_pool(name="psum", bufs=1))
+        ctx.enter_context(tc.manual_schedule())
+
+        def rows(ap):
+            return ap.rearrange("(p t) d -> p t d", t=TILES)
+
+        x_sb, state_sb = {}, {}
+
+        def load_x(t0, n):
+            xt = keep.tile([P, n, DI], BF16, name="x%d" % t0, align_bytes=64)
+            nc.sync.dma_start(out=xt[:], in_=rows(x)[:, t0 : t0 + n, :])
+            for i in range(n):
+                x_sb[t0 + i] = xt[:, i, :]
+
+        def load_state(key, src, t0, n):
+            st = keep.tile([P, n, DH], BF16, name="%s%d" % (key, t0), align_bytes=64)
+            nc.sync.dma_start(out=st[:], in_=rows(src)[:, t0 : t0 + n, :])
+            for i in range(n):
+                state_sb[key, t0 + i] = st[:, i, :]
+
+        def load_words(name, c0, c1):
+            wt = keep.tile([P, PASSES, 2 * (c1 - c0)], U8, name=name, align_bytes=64)
+            src = weight_ih_words.rearrange("g p n -> p g n")[:, :, 2 * c0 : 2 * c1]
+            nc.sync.dma_start(out=wt[:].bitcast(I32), in_=src.bitcast(I32))
+            return wt
+
+        plane = keep.tile([P, PASSES, NG], U8, name="plane", align_bytes=64)
+        nc.vector.memset(plane[:].bitcast(I32), 0)
+
+        bias_rows = keep.tile([P, 2, P], BF16, name="bias_rows", align_bytes=64)
+        ident_f = keep.tile([P, P], F32, name="ident_f", align_bytes=64)
+        ident_b = keep.tile([P, P], BF16, name="ident_b", align_bytes=64)
+        mask_sb = keep.tile([P, TILES], BF16, name="mask_sb")
+        nc.gpsimd.memset(bias_rows[:], 0.0)
+        make_identity(nc, ident_f[:])
+        nc.vector.tensor_copy(out=ident_b[:], in_=ident_f[:])
+        nc.scalar.dma_start(out=bias_rows[0:BLOCKS, 0, :], in_=bias_ih.rearrange("(j p) -> j p", p=P))
+        nc.scalar.dma_start(out=bias_rows[OTHER_BIAS_ROW : OTHER_BIAS_ROW + HH_BLOCKS, 0, :],
+                            in_=bias_hh.rearrange("(j p) -> j p", p=P))
+        for i, vec in enumerate((bias_sh0, bias_sh1, bias_sh2)):
+            nc.gpsimd.dma_start(out=bias_rows[2 * i : 2 * i + 2, 1, :], in_=vec.rearrange("(j p) -> j p", p=P))
+        nc.gpsimd.dma_start(out=mask_sb[:], in_=mask.rearrange("(p t) -> p t", t=TILES))
+
+        load_x(0, 1)
+        load_x(1, 1)
+        whh_raw = keep.tile([P, HH_BLOCKS, DH], BF16, name="whh_raw", align_bytes=64)
+        nc.sync.dma_start(out=whh_raw[:], in_=weight_hh.rearrange("(j p) k -> p j k", p=P))
+        for q in range(4):
+            nc.sync.dma_start(
+                out=plane[32 * q : 32 * q + 4, :, :].bitcast(I32),
+                in_=weight_ih_scales[:, 4 * q : 4 * q + 4, :].rearrange("g r n -> r g n").bitcast(I32),
+            )
+        words_hh = load_words("words_hh", 0, 4 * DH)
+        states = (("h", h_minors), ("s0", s0), ("s1", s1), ("s2", s2))
+        for key, src in states:
+            load_state(key, src, 0, 2)
+        load_x(2, 2)
+        words_s = load_words("words_s", 4 * DH, NG)
+        wsh_raw = []
+        for i, w in enumerate((weight_sh0, weight_sh1, weight_sh2)):
+            wr = keep.tile([P, 2, DH], BF16, name="wsh_raw%d" % i, align_bytes=64)
+            nc.sync.dma_start(out=wr[:], in_=w.rearrange("(j p) k -> p j k", p=P))
+            wsh_raw.append(wr)
+        load_state("c", c_minors, 0, 2)
+        for key, src in states:
+            load_state(key, src, 2, TILES - 2)
+        load_x(4, 2)
+        load_state("c", c_minors, 2, TILES - 2)
+        load_x(6, 2)
+
+        wt_hh = keep.tile([P, 2, 4 * DH], BF16, name="wt_hh", align_bytes=64)
+        wt_s = keep.tile([P, 2, 3 * DH], BF16, name="wt_s", align_bytes=64)
+        bias_two = keep.tile([P, 32], F32, name="bias_two")
+        bias_hh_col = keep.tile([P, HH_BLOCKS], F32, name="bias_hh_col")
+        bias_s_col = keep.tile([P, BLOCKS - HH_BLOCKS], F32, name="bias_s_col")
+        m1 = keep.tile([P, TILES], F32, name="m1")
+        m2 = keep.tile([P, TILES], F32, name="m2")
+        m3 = keep.tile([P, TILES], F32, name="m3")
+
+        grouped, codes, scales, mx_sb, hs_t, gates, tanh_c, outs, banks = {}, {}, {}, {}, {}, {}, {}, {}, {}
+        xt_ps, hs_ps, mx_ps = {}, {}, {}
+
+        def copy_on(engine, out, in_):
+            if engine == "act":
+                nc.scalar.copy(out=out, in_=in_)
+            else:
+                nc.vector.tensor_copy(out=out, in_=in_)
+
+        def x_transpose(t, i):
+            g, u = divmod(i, 2)
+            if i == 0:
+                xt_ps[t] = psum.tile([P, PASSES, 2, P], F32, name="xt_ps", tag="tr", bufs=2)
+            words = x_sb[t].bitcast(F32)
+            nc.tensor.transpose(xt_ps[t][:, g, u, :], words[:, 256 * g + u : 256 * (g + 1) : 2], ident_f[:])
+
+        def x_copy(t, engine):
+            s, tt = divmod(t, 2)
+            if tt == 0:
+                grouped[s] = work.tile([P, PASSES, 2, P, 2], F32, name="grouped", align_bytes=64)
+            copy_on(engine, grouped[s][:, :, tt, :, :], xt_ps[t][:].rearrange("p g u r -> p g r u"))
+
+        def quantize(s):
+            codes[s] = work.tile([P, PASSES * PAIR_ROWS], U32, name="codes", bufs=3, align_bytes=64)
+            scales[s] = work.tile([P, PASSES * PAIR_ROWS], U8, name="scales", bufs=3, align_bytes=64)
+            nc.vector.quantize_mx(
+                out=codes[s][:].bitcast(E5M2X4),
+                scales=scales[s][:],
+                in_=grouped[s][:].rearrange("p g t r u -> p (g t r u)").bitcast(BF16),
+            )
+
+        def hs_transpose(t, i):
+            if i == 0:
+                hs_ps[t] = psum.tile([P, 8, P], BF16, name="hs_ps", tag="tr", bufs=2)
+            key, c = states[i // 2][0], i % 2
+            nc.tensor.transpose(hs_ps[t][:, i, :], state_sb[key, t][:, P * c : P * (c + 1)], ident_b[:])
+
+        def hs_copy(t, engine):
+            hs_t[t] = work.tile([P, 8, P], BF16, name="hs_t", align_bytes=64)
+            copy_on(engine, hs_t[t][:], hs_ps[t][:])
+
+        def mx_pair(s, pair):
+            ps = psum.tile([P, 2, PAIR_ROWS], F32, name="mx_ps", tag="mx", bufs=2)
+            mx_ps[s, pair] = ps
+            for i, j in enumerate(pair):
+                words, jj = (words_hh, j) if j < HH_BLOCKS else (words_s, j - HH_BLOCKS)
+                for g in range(PASSES):
+                    nc.tensor.matmul_mx(
+                        out=ps[:, i, :],
+                        lhsT=words[:, g, 2 * P * jj : 2 * P * (jj + 1)].bitcast(E2M1X4),
+                        lhsT_scale=plane[:, g, P * j : P * (j + 1)],
+                        rhs=codes[s][:, PAIR_ROWS * g : PAIR_ROWS * (g + 1)].bitcast(E5M2X4),
+                        rhs_scale=scales[s][:, PAIR_ROWS * g : PAIR_ROWS * (g + 1)],
+                        start=(g == 0),
+                        stop=(g == PASSES - 1),
+                    )
+
+        def mx_copy(s, pair, engine):
+            sb = work.tile([P, 2, PAIR_ROWS], F32, name="mx_sb", bufs=BLOCKS, align_bytes=64)
+            ps = mx_ps[s, pair]
+            for i, j in enumerate(pair):
+                mx_sb[s, j] = sb[:, i, :]
+            bias_col, first = (bias_hh_col, 0) if pair[0] < HH_BLOCKS else (bias_s_col, HH_BLOCKS)
+            j0, j1 = pair[0] - first, pair[1] - first
+            if engine == "act":
+                for i, j in enumerate((j0, j1)):
+                    nc.scalar.activation(out=sb[:, i, :], in_=ps[:, i, :], func=ACT.Identity, bias=bias_col[:, j : j + 1])
+            else:
+                both = bias_col[:, j0 : j1 + 1 : j1 - j0].unsqueeze(2).to_broadcast([P, 2, PAIR_ROWS])
+                nc.vector.tensor_tensor(out=sb[:], in0=ps[:], in1=both, op=ALU.add)
+
+        def bank_of(j):
+            if j < HH_BLOCKS:
+                return ("gA", "gB")[j // 4], j % 4
+            return ("gC", "gD")[(j - HH_BLOCKS) // 3], (j - HH_BLOCKS) % 3
+
+        def gate_group(t, j, between):
+            s, tt = divmod(t, 2)
+            tag, q = bank_of(j)
+            if q == 0:
+                banks[t, tag] = psum.tile([P, 4 * P], F32, name=tag, tag=tag)
+            out = banks[t, tag][:, P * q : P * (q + 1)]
+            if j < HH_BLOCKS:
+                first, wt, jj = 0, wt_hh, j
+            else:
+                first, wt, jj = 2 + 2 * ((j - HH_BLOCKS) // 2), wt_s, j - HH_BLOCKS
+            nc.tensor.matmul(out, lhsT=mx_sb[s, j][:, P * tt : P * (tt + 1)], rhs=ident_f[:],
+                             is_transpose=True, start=True, stop=False)
+            nc.tensor.matmul(out, lhsT=hs_t[t][:, first, :], rhs=wt[:, 0, P * jj : P * (jj + 1)], start=False, stop=False)
+            between()
+            nc.tensor.matmul(out, lhsT=hs_t[t][:, first + 1, :], rhs=wt[:, 1, P * jj : P * (jj + 1)], start=False, stop=True)
+
+        def gate(t, n, count=1):
+            return gates[t][:, DH * n : DH * (n + count)]
+
+        def act_if(t):
+            gates[t] = work.tile([P, NG], F32, name="gates", bufs=3, align_bytes=64)
+            nc.scalar.activation(out=gate(t, 0, 2), in_=banks[t, "gA"][:], func=ACT.Sigmoid)
+
+        def act_go(t):
+            nc.scalar.activation(out=gate(t, 2), in_=banks[t, "gB"][:, DH:], func=ACT.Tanh)
+            nc.scalar.activation(out=gate(t, 3), in_=banks[t, "gB"][:, :DH], func=ACT.Sigmoid)
+
+        def act_shared(t, half):
+            w = 3 * P
+            c0 = 4 * DH + w * half
+            nc.scalar.activation(out=gates[t][:, c0 : c0 + w], in_=banks[t, ("gC", "gD")[half]][:, :w], func=ACT.Sigmoid)
+
+        def act_tanh_c(t):
+            tanh_c[t] = work.tile([P, DH], F32, name="tanh_c", align_bytes=64)
+            nc.scalar.activation(out=tanh_c[t][:], in_=out_slot(t, 0), func=ACT.Tanh)
+
+        def out_slot(t, n):
+            return outs[t // 2][:, n, t % 2, :]
+
+        def stt(out, in0, scalar, in1, op0, op1):
+            nc.vector.scalar_tensor_tensor(out=out, in0=in0, scalar=scalar, in1=in1, op0=op0, op1=op1)
+
+        def step(name, t):
+            col = slice(t, t + 1)
+            if name == "fc":
+                stt(gate(t, 1), gate(t, 1), m1[:, col], state_sb["c", t], ALU.mult, ALU.mult)
+            elif name == "ig":
+                stt(gate(t, 0), gate(t, 0), m1[:, col], gate(t, 2), ALU.mult, ALU.mult)
+            elif name == "ct":
+                if t % 2 == 0:
+                    outs[t // 2] = work.tile([P, 5, 2, DH], F32, name="outs", bufs=3, align_bytes=64)
+                nc.vector.tensor_tensor(out=out_slot(t, 0), in0=gate(t, 0), in1=gate(t, 1), op=ALU.add)
+            elif name in ("d0", "d1", "d2"):
+                n = int(name[1])
+                stt(gate(t, 4 + n), gate(t, 4 + n), float(n + 1), gate(t, 3), ALU.add, ALU.subtract)
+            elif name == "hs0":
+                th = tanh_c[t][:].unsqueeze(1).to_broadcast([P, 2, DH])
+                stt(outs[t // 2][:, 1:3, t % 2, :], th, m1[:, col],
+                    gate(t, 3, 2).rearrange("p (a d) -> p a d", a=2), ALU.mult, ALU.mult)
+            elif name == "e1":
+                nc.vector.tensor_tensor(out=gate(t, 5), in0=gate(t, 5), in1=out_slot(t, 2), op=ALU.subtract)
+            elif name == "f2":
+                stt(gate(t, 6), out_slot(t, 2), -2.0, gate(t, 6), ALU.mult, ALU.add)
+            elif name == "s1":
+                stt(out_slot(t, 3), tanh_c[t][:], m2[:, col], gate(t, 5), ALU.mult, ALU.mult)
+            elif name == "e2":
+                nc.vector.tensor_tensor(out=gate(t, 6), in0=gate(t, 6), in1=out_slot(t, 3), op=ALU.subtract)
+            else:
+                stt(out_slot(t, 4), tanh_c[t][:], m3[:, col], gate(t, 6), ALU.mult, ALU.mult)
+
+        out_of_slot = (out_1, out_0, out_2, out_3, out_4)
+
+        def store(t, slots):
+            last_pair = t // 2 == TILES // 2 - 1
+            for n in slots:
+                if last_pair:
+                    nc.sync.dma_start(out=rows(out_of_slot[n])[:, t, :], in_=out_slot(t, n))
+                elif t % 2 == 1:
+                    nc.sync.dma_start(out=rows(out_of_slot[n])[:, t - 1 : t + 1, :], in_=outs[t // 2][:, n, :, :])
+
+        def weight_transposes(tag, wt, c, block, count, engine):
+            ps = psum.tile([P, count, P], BF16, name="wt_ps", tag=tag)
+            for j in range(count):
+                nc.tensor.matmul(ps[:, j, :], lhsT=block(j)[:, P * c : P * (c + 1)], rhs=ident_b[:], start=True, stop=True)
+            copy_on(engine, wt[:, c, :], ps[:].rearrange("p j n -> p (j n)"))
+
+        def bias_transpose(half):
+            ps = psum.tile([P, P], BF16, name="bias_ps", tag="tr", bufs=2)
+            nc.tensor.transpose(ps[:], bias_rows[:, half, :], ident_b[:])
+            if half == 0:
+                nc.vector.tensor_copy(out=bias_two[:], in_=ps[:, 0:32])
+                nc.vector.tensor_tensor(out=bias_hh_col[:], in0=bias_two[:, 0:HH_BLOCKS],
+                                        in1=bias_two[:, OTHER_BIAS_ROW : OTHER_BIAS_ROW + HH_BLOCKS], op=ALU.add)
+            else:
+                nc.vector.tensor_tensor(out=bias_s_col[:], in0=ps[:, 0 : BLOCKS - HH_BLOCKS],
+                                        in1=bias_two[:, HH_BLOCKS:BLOCKS], op=ALU.add)
+
+        for t, engine in ((0, "dve"), (1, "act")):
+            for i in range(4):
+                x_transpose(t, i)
+            x_copy(t, engine)
+        bias_transpose(0)
+        quantize(0)
+        for c in range(2):
+            weight_transposes(("gA", "gB")[c], wt_hh, c, lambda j: whh_raw[:, j, :], HH_BLOCKS, "act")
+        mx_pair(0, HH_PAIRS[0])
+        mx_copy(0, HH_PAIRS[0], "dve")
+        for i in range(8):
+            hs_transpose(0, i)
+        hs_copy(0, "act")
+        mx_pair(0, HH_PAIRS[1])
+        mx_copy(0, HH_PAIRS[1], "dve")
+        bias_transpose(1)
+        for m, factor in ((m1, 1.0), (m2, 0.5), (m3, 1.0 / 3.0)):
+            nc.vector.tensor_scalar(out=m[:], in0=mask_sb[:], scalar1=factor, scalar2=None, op0=ALU.mult)
+
+        all_pairs = [(s, pair) for s in range(TILES // 2) for pair in HH_PAIRS + S_PAIRS]
+        done = 2
+        for t in range(TILES):
+            r = t - 1
+            slots = PAIR_SLOTS[t]
+            pairs = dict(zip(slots, all_pairs[done : done + len(slots)]))
+            done += len(slots)
+            if r >= 0:
+                step("d0", r)
+                step("d1", r)
+            for k, j in enumerate(BLOCK_ORDER):
+                gate_group(t, j, (lambda a=pairs.get(k): mx_pair(*a) if a else None))
+                if k == 0 and r >= 0:
+                    act_tanh_c(r)
+                    for name in ("hs0", "d2"):
+                        step(name, r)
+                    if t in (2, 3):
+                        quantize(t)
+                    for name in ("e1", "f2", "s1"):
+                        step(name, r)
+                    store(r, (0, 1, 2, 3))
+                if k == 6:
+                    act_if(t)
+                if k == 12:
+                    act_shared(t, 0)
+                if k in pairs:
+                    mx_copy(*pairs[k], "dve" if t == 0 else "act")
+                if t == 0:
+                    if k in (1, 3):
+                        weight_transposes(("gC", "gD")[k // 2], wt_s, k // 2, lambda j: wsh_raw[j // 2][:, j % 2, :], 6, "dve")
+                    if 2 <= k < 10:
+                        x_transpose(2 + (k - 2) // 4, (k - 2) % 4)
+                    if k in (5, 9):
+                        x_copy(2 + k // 9, "dve")
+                    if k == 9:
+                        quantize(1)
+                if t + 1 < TILES and k < 4:
+                    hs_transpose(t + 1, 2 * k)
+                    hs_transpose(t + 1, 2 * k + 1)
+                    if k == 3:
+                        hs_copy(t + 1, "act")
+                if t in (1, 2) and 4 <= k < 12:
+                    x_transpose(2 * t + 2 + (k - 4) // 4, k % 4)
+                    if k == 7:
+                        x_copy(2 * t + 2, "dve")
+                if k == 7:
+                    act_go(t)
+                if k == (9 if t == 0 else 7):
+                    step("fc", t)
+                    if r >= 0:
+                        step("e2", r)
+                    step("ig", t)
+                    if r >= 0:
+                        step("s2", r)
+                        store(r, (4,))
+                    step("ct", t)
+                if k == 11 and t in (1, 2):
+                    x_copy(2 * t + 3, "dve")
+                if k == 13:
+                    act_shared(t, 1)
+        r = TILES - 1
+        act_tanh_c(r)
+        store(r, (0,))
+        for name in ("d0", "d1", "hs0", "d2", "e1", "f2", "s1", "e2", "s2"):
+            step(name, r)
+            if name == "hs0":
+                store(r, (1, 2))
+            if name == "s1":
+                store(r, (3,))
+        store(r, (4,))

@@ -20,14 +20,14 @@ ALU = mybir.AluOpType
 P = 128
 TILES = B // P
 PASSES = DI // 512
-BLOCKS = NG // P
 HH_BLOCKS = 4 * DH // P
 PAIR_ROWS = 2 * P
-HH_PAIRS = [(0, 4), (1, 5), (2, 6), (3, 7)]
-S_PAIRS = [(8, 11), (9, 12), (10, 13)]
-BLOCK_ORDER = [j for pair in HH_PAIRS + S_PAIRS for j in pair]
-OTHER_BIAS_ROW = 16
-PAIR_SLOTS = [(0, 2, 4, 6, 8)] + [(2, 5, 8, 11), (0, 3, 6)] * 3 + [()]
+PAIRS = [(0, 2), (1, 3), (6, 8), (7, 9), (4, 5)]
+T_BLOCKS = 10
+T_COLS = T_BLOCKS * P
+A_COLS = NG - T_COLS
+CHUNKS = [(0, 512), (512, 1024), (1024, T_COLS), (T_COLS, NG)]
+SH = 3 * DH
 
 
 def tile_share_lstm_cell_pa_kernel(
@@ -68,41 +68,43 @@ def tile_share_lstm_cell_pa_kernel(
         plane = keep.tile([P, PASSES, NG], U8, name="plane", align_bytes=64)
         nc.vector.memset(plane[:].bitcast(I32), 0)
 
-        bias_rows = keep.tile([P, 2, P], BF16, name="bias_rows", align_bytes=64)
+        bias_rows = keep.tile([P, NG], BF16, name="bias_rows", align_bytes=64)
+        ones = keep.tile([P, P], BF16, name="ones", align_bytes=64)
         ident_f = keep.tile([P, P], F32, name="ident_f", align_bytes=64)
         ident_b = keep.tile([P, P], BF16, name="ident_b", align_bytes=64)
         mask_sb = keep.tile([P, TILES], BF16, name="mask_sb")
-        nc.gpsimd.memset(bias_rows[:], 0.0)
         make_identity(nc, ident_f[:])
+        nc.vector.memset(bias_rows[:].bitcast(I32), 0)
+        nc.vector.memset(ones[:], 1.0)
         nc.vector.tensor_copy(out=ident_b[:], in_=ident_f[:])
-        nc.scalar.dma_start(out=bias_rows[0:BLOCKS, 0, :], in_=bias_ih.rearrange("(j p) -> j p", p=P))
-        nc.scalar.dma_start(out=bias_rows[OTHER_BIAS_ROW : OTHER_BIAS_ROW + HH_BLOCKS, 0, :],
-                            in_=bias_hh.rearrange("(j p) -> j p", p=P))
         for i, vec in enumerate((bias_sh0, bias_sh1, bias_sh2)):
-            nc.gpsimd.dma_start(out=bias_rows[2 * i : 2 * i + 2, 1, :], in_=vec.rearrange("(j p) -> j p", p=P))
+            nc.gpsimd.dma_start(out=bias_rows[1:2, DH * (4 + i) : DH * (5 + i)], in_=vec.rearrange("(a n) -> a n", a=1))
         nc.gpsimd.dma_start(out=mask_sb[:], in_=mask.rearrange("(p t) -> p t", t=TILES))
 
+        states = (("h", h_minors), ("s0", s0), ("s1", s1), ("s2", s2))
         load_x(0, 1)
-        load_x(1, 1)
         whh_raw = keep.tile([P, HH_BLOCKS, DH], BF16, name="whh_raw", align_bytes=64)
         nc.sync.dma_start(out=whh_raw[:], in_=weight_hh.rearrange("(j p) k -> p j k", p=P))
+        load_state("h", h_minors, 0, 2)
+        words_hh = load_words("words_hh", 0, T_COLS)
         for q in range(4):
             nc.sync.dma_start(
                 out=plane[32 * q : 32 * q + 4, :, :].bitcast(I32),
                 in_=weight_ih_scales[:, 4 * q : 4 * q + 4, :].rearrange("g r n -> r g n").bitcast(I32),
             )
-        words_hh = load_words("words_hh", 0, 4 * DH)
-        states = (("h", h_minors), ("s0", s0), ("s1", s1), ("s2", s2))
-        for key, src in states:
+        nc.scalar.dma_start(out=bias_rows[0:1, :], in_=bias_ih.rearrange("(a n) -> a n", a=1))
+        nc.scalar.dma_start(out=bias_rows[1:2, : 4 * DH], in_=bias_hh.rearrange("(a n) -> a n", a=1))
+        load_x(1, 1)
+        for key, src in states[1:]:
             load_state(key, src, 0, 2)
-        load_x(2, 2)
-        words_s = load_words("words_s", 4 * DH, NG)
         wsh_raw = []
         for i, w in enumerate((weight_sh0, weight_sh1, weight_sh2)):
             wr = keep.tile([P, 2, DH], BF16, name="wsh_raw%d" % i, align_bytes=64)
             nc.sync.dma_start(out=wr[:], in_=w.rearrange("(j p) k -> p j k", p=P))
             wsh_raw.append(wr)
+        words_s = load_words("words_s", T_COLS, NG)
         load_state("c", c_minors, 0, 2)
+        load_x(2, 2)
         for key, src in states:
             load_state(key, src, 2, TILES - 2)
         load_x(4, 2)
@@ -111,15 +113,14 @@ def tile_share_lstm_cell_pa_kernel(
 
         wt_hh = keep.tile([P, 2, 4 * DH], BF16, name="wt_hh", align_bytes=64)
         wt_s = keep.tile([P, 2, 3 * DH], BF16, name="wt_s", align_bytes=64)
-        bias_two = keep.tile([P, 32], F32, name="bias_two")
-        bias_hh_col = keep.tile([P, HH_BLOCKS], F32, name="bias_hh_col")
-        bias_s_col = keep.tile([P, BLOCKS - HH_BLOCKS], F32, name="bias_s_col")
+        bias_hh_col = keep.tile([P, T_BLOCKS], F32, name="bias_hh_col")
+        bias_all = keep.tile([P, NG], F32, name="bias_all", align_bytes=64)
         m1 = keep.tile([P, TILES], F32, name="m1")
         m2 = keep.tile([P, TILES], F32, name="m2")
         m3 = keep.tile([P, TILES], F32, name="m3")
 
         grouped, codes, scales, mx_sb, hs_t, gates, tanh_c, outs, banks = {}, {}, {}, {}, {}, {}, {}, {}, {}
-        xt_ps, hs_ps, mx_ps = {}, {}, {}
+        xt_ps, hs_ps, mx_ps, pre = {}, {}, {}, {}
 
         def copy_on(engine, out, in_):
             if engine == "act":
@@ -130,101 +131,159 @@ def tile_share_lstm_cell_pa_kernel(
         def x_transpose(t, i):
             g, u = divmod(i, 2)
             if i == 0:
-                xt_ps[t] = psum.tile([P, PASSES, 2, P], F32, name="xt_ps", tag="tr", bufs=2)
+                xt_ps[t] = psum.tile([P, PASSES, 2, P], F32, name="xt_ps", tag="rot", bufs=3)
             words = x_sb[t].bitcast(F32)
             nc.tensor.transpose(xt_ps[t][:, g, u, :], words[:, 256 * g + u : 256 * (g + 1) : 2], ident_f[:])
 
-        def x_copy(t, engine):
-            s, tt = divmod(t, 2)
-            if tt == 0:
-                grouped[s] = work.tile([P, PASSES, 2, P, 2], F32, name="grouped", align_bytes=64)
-            copy_on(engine, grouped[s][:, :, tt, :, :], xt_ps[t][:].rearrange("p g u r -> p g r u"))
+        def unit_of(t):
+            return ((t, 1), 0) if t < 2 else ((t - t % 2, 2), t % 2)
 
-        def quantize(s):
-            codes[s] = work.tile([P, PASSES * PAIR_ROWS], U32, name="codes", bufs=3, align_bytes=64)
-            scales[s] = work.tile([P, PASSES * PAIR_ROWS], U8, name="scales", bufs=3, align_bytes=64)
+        def x_copy(t, engine):
+            unit, tt = unit_of(t)
+            if tt == 0:
+                grouped[unit] = work.tile([P, PASSES, unit[1], P, 2], F32, name="grouped", align_bytes=64)
+            copy_on(engine, grouped[unit][:, :, tt, :, :], xt_ps[t][:].rearrange("p g u r -> p g r u"))
+
+        def quantize(t):
+            unit = unit_of(t)[0]
+            codes[unit] = work.tile([P, PASSES, unit[1] * P], U32, name="codes", bufs=3, align_bytes=64)
+            scales[unit] = work.tile([P, PASSES, unit[1] * P], U8, name="scales", bufs=3, align_bytes=64)
             nc.vector.quantize_mx(
-                out=codes[s][:].bitcast(E5M2X4),
-                scales=scales[s][:],
-                in_=grouped[s][:].rearrange("p g t r u -> p (g t r u)").bitcast(BF16),
+                out=codes[unit][:].rearrange("p g c -> p (g c)").bitcast(E5M2X4),
+                scales=scales[unit][:].rearrange("p g c -> p (g c)"),
+                in_=grouped[unit][:].rearrange("p g t r u -> p (g t r u)").bitcast(BF16),
             )
 
-        def hs_transpose(t, i):
-            if i == 0:
-                hs_ps[t] = psum.tile([P, 8, P], BF16, name="hs_ps", tag="tr", bufs=2)
-            key, c = states[i // 2][0], i % 2
-            nc.tensor.transpose(hs_ps[t][:, i, :], state_sb[key, t][:, P * c : P * (c + 1)], ident_b[:])
+        def hs_transposes(t, first=0, last=4):
+            hs_ps[t] = psum.tile([P, 4, P], F32, name="hs_ps", tag="rot", bufs=3)
+            for i in range(first, last):
+                nc.tensor.transpose(hs_ps[t][:, i, :], state_sb[states[i][0], t].bitcast(F32), ident_f[:])
 
-        def hs_copy(t, engine):
-            hs_t[t] = work.tile([P, 8, P], BF16, name="hs_t", align_bytes=64)
-            copy_on(engine, hs_t[t][:], hs_ps[t][:])
+        def hs_copy(t, engine, first=0, last=4):
+            if first == 0:
+                hs_t[t] = work.tile([P, 4, P], F32, name="hs_t", align_bytes=64)
+            copy_on(engine, hs_t[t][:, first:last, :], hs_ps[t][:, first:last, :])
+
+        def state_t(t, i, e):
+            return hs_t[t][:, i, :].bitcast(BF16)[:, e :: 2]
 
         def mx_pair(s, pair):
-            ps = psum.tile([P, 2, PAIR_ROWS], F32, name="mx_ps", tag="mx", bufs=2)
+            ps = psum.tile([P, 2, PAIR_ROWS], F32, name="mx_ps", tag="rot", bufs=3)
             mx_ps[s, pair] = ps
             for i, j in enumerate(pair):
-                words, jj = (words_hh, j) if j < HH_BLOCKS else (words_s, j - HH_BLOCKS)
                 for g in range(PASSES):
                     nc.tensor.matmul_mx(
                         out=ps[:, i, :],
-                        lhsT=words[:, g, 2 * P * jj : 2 * P * (jj + 1)].bitcast(E2M1X4),
+                        lhsT=words_hh[:, g, 2 * P * j : 2 * P * (j + 1)].bitcast(E2M1X4),
                         lhsT_scale=plane[:, g, P * j : P * (j + 1)],
-                        rhs=codes[s][:, PAIR_ROWS * g : PAIR_ROWS * (g + 1)].bitcast(E5M2X4),
-                        rhs_scale=scales[s][:, PAIR_ROWS * g : PAIR_ROWS * (g + 1)],
+                        rhs=codes[2 * s, 2][:, g, :].bitcast(E5M2X4),
+                        rhs_scale=scales[2 * s, 2][:, g, :],
                         start=(g == 0),
                         stop=(g == PASSES - 1),
                     )
 
         def mx_copy(s, pair, engine):
-            sb = work.tile([P, 2, PAIR_ROWS], F32, name="mx_sb", bufs=BLOCKS, align_bytes=64)
+            sb = work.tile([P, 2, PAIR_ROWS], F32, name="mx_sb", bufs=10, align_bytes=64)
             ps = mx_ps[s, pair]
+            j0, j1 = pair
             for i, j in enumerate(pair):
                 mx_sb[s, j] = sb[:, i, :]
-            bias_col, first = (bias_hh_col, 0) if pair[0] < HH_BLOCKS else (bias_s_col, HH_BLOCKS)
-            j0, j1 = pair[0] - first, pair[1] - first
             if engine == "act":
-                for i, j in enumerate((j0, j1)):
-                    nc.scalar.activation(out=sb[:, i, :], in_=ps[:, i, :], func=ACT.Identity, bias=bias_col[:, j : j + 1])
+                for i, j in enumerate(pair):
+                    nc.scalar.activation(out=sb[:, i, :], in_=ps[:, i, :], func=ACT.Identity, bias=bias_hh_col[:, j : j + 1])
             else:
-                both = bias_col[:, j0 : j1 + 1 : j1 - j0].unsqueeze(2).to_broadcast([P, 2, PAIR_ROWS])
+                both = bias_hh_col[:, j0 : j1 + 1 : j1 - j0].unsqueeze(2).to_broadcast([P, 2, PAIR_ROWS])
                 nc.vector.tensor_tensor(out=sb[:], in0=ps[:], in1=both, op=ALU.add)
 
-        def bank_of(j):
-            if j < HH_BLOCKS:
-                return ("gA", "gB")[j // 4], j % 4
-            return ("gC", "gD")[(j - HH_BLOCKS) // 3], (j - HH_BLOCKS) % 3
-
-        def gate_group(t, j, between):
+        def open_group(t, j, tag, q):
             s, tt = divmod(t, 2)
-            tag, q = bank_of(j)
             if q == 0:
                 banks[t, tag] = psum.tile([P, 4 * P], F32, name=tag, tag=tag)
-            out = banks[t, tag][:, P * q : P * (q + 1)]
-            if j < HH_BLOCKS:
-                first, wt, jj = 0, wt_hh, j
+            nc.tensor.matmul(banks[t, tag][:, P * q : P * (q + 1)], lhsT=mx_sb[s, j][:, P * tt : P * (tt + 1)],
+                             rhs=ident_f[:], is_transpose=True, start=True, stop=False)
+
+        def plain_pass(t, j, tag, q, e):
+            state, wt, jj = (0, wt_hh, j) if j < HH_BLOCKS else (1, wt_s, j - HH_BLOCKS)
+            nc.tensor.matmul(banks[t, tag][:, P * q : P * (q + 1)], lhsT=state_t(t, state, e),
+                             rhs=wt[:, e, P * jj : P * (jj + 1)], start=False, stop=(e == 1))
+
+        def gate_round(t, q, between):
+            blocks = list(zip(PAIRS[q], ("gA", "gB")))
+            for j, tag in blocks:
+                open_group(t, j, tag, q)
+            for e in range(2):
+                for j, tag in blocks:
+                    plain_pass(t, j, tag, q, e)
+                if e == 0:
+                    between()
+
+        def o_group(t, q):
+            j = PAIRS[4][q]
+            open_group(t, j, "gC", q)
+            for e in range(2):
+                plain_pass(t, j, "gC", q, e)
+
+        def chunk_products(t, c, tags, between):
+            unit, tt = unit_of(t)
+            c0, c1 = CHUNKS[c]
+            if len(tags) == 2:
+                mx_out = psum.tile([P, c1 - c0], F32, name="mx_out", tag=tags[0])[:]
+                plain_out = psum.tile([P, c1 - c0], F32, name="plain_out", tag=tags[1])[:]
             else:
-                first, wt, jj = 2 + 2 * ((j - HH_BLOCKS) // 2), wt_s, j - HH_BLOCKS
-            nc.tensor.matmul(out, lhsT=mx_sb[s, j][:, P * tt : P * (tt + 1)], rhs=ident_f[:],
-                             is_transpose=True, start=True, stop=False)
-            nc.tensor.matmul(out, lhsT=hs_t[t][:, first, :], rhs=wt[:, 0, P * jj : P * (jj + 1)], start=False, stop=False)
+                both = psum.tile([P, 2, c1 - c0], F32, name="both_out", tag=tags[0])
+                mx_out, plain_out = both[:, 0, :], both[:, 1, :]
+            banks[t, c] = (mx_out, plain_out)
+            words, w0 = (words_hh, 0) if c1 <= T_COLS else (words_s, T_COLS)
+            for g in range(PASSES):
+                nc.tensor.matmul_mx(
+                    out=mx_out,
+                    lhsT=codes[unit][:, g, P * tt : P * (tt + 1)].bitcast(E5M2X4),
+                    lhsT_scale=scales[unit][:, g, P * tt : P * (tt + 1)],
+                    rhs=words[:, g, 2 * (c0 - w0) : 2 * (c1 - w0)].bitcast(E2M1X4),
+                    rhs_scale=plane[:, g, c0:c1],
+                    start=(g == 0),
+                    stop=(g == PASSES - 1),
+                )
             between()
-            nc.tensor.matmul(out, lhsT=hs_t[t][:, first + 1, :], rhs=wt[:, 1, P * jj : P * (jj + 1)], start=False, stop=True)
+            if c1 <= 4 * DH:
+                parts = [(0, wt_hh, c0, c1, 0)]
+            else:
+                parts = [(n - 3, wt_s, DH * (n - 4), DH * (n - 3), DH * n - c0) for n in range(c0 // DH, c1 // DH)]
+            for state, wt, w0, w1, o0 in parts:
+                for e in range(2):
+                    nc.tensor.matmul(plain_out[:, o0 : o0 + w1 - w0], lhsT=state_t(t, state, e), rhs=wt[:, e, w0:w1],
+                                     start=(e == 0), stop=(e == 1))
+
+        def chunk_sum(name, t, c):
+            c0, c1 = CHUNKS[c]
+            if name == "p":
+                pre[t, c] = work.tile([P, c1 - c0], F32, name="pre", bufs=4, align_bytes=64)
+                nc.vector.tensor_tensor(out=pre[t, c][:], in0=banks[t, c][0], in1=bias_all[:, c0:c1], op=ALU.add)
+            else:
+                nc.vector.tensor_tensor(out=pre[t, c][:], in0=banks[t, c][1], in1=pre[t, c][:], op=ALU.add)
 
         def gate(t, n, count=1):
             return gates[t][:, DH * n : DH * (n + count)]
 
-        def act_if(t):
+        def act_first(t):
             gates[t] = work.tile([P, NG], F32, name="gates", bufs=3, align_bytes=64)
-            nc.scalar.activation(out=gate(t, 0, 2), in_=banks[t, "gA"][:], func=ACT.Sigmoid)
+            nc.scalar.activation(out=gate(t, 0), in_=banks[t, "gA"][:, :DH], func=ACT.Sigmoid)
+            nc.scalar.activation(out=gate(t, 2), in_=banks[t, "gA"][:, DH:], func=ACT.Tanh)
+            f_and_b0 = gates[t][:].rearrange("p (a d) -> p a d", d=DH)[:, 1:5:3, :]
+            nc.scalar.activation(out=f_and_b0, in_=banks[t, "gB"][:].rearrange("p (a d) -> p a d", d=DH), func=ACT.Sigmoid)
 
-        def act_go(t):
-            nc.scalar.activation(out=gate(t, 2), in_=banks[t, "gB"][:, DH:], func=ACT.Tanh)
-            nc.scalar.activation(out=gate(t, 3), in_=banks[t, "gB"][:, :DH], func=ACT.Sigmoid)
+        def act_o(t):
+            nc.scalar.activation(out=gate(t, 3), in_=banks[t, "gC"][:, :DH], func=ACT.Sigmoid)
 
-        def act_shared(t, half):
-            w = 3 * P
-            c0 = 4 * DH + w * half
-            nc.scalar.activation(out=gates[t][:, c0 : c0 + w], in_=banks[t, ("gC", "gD")[half]][:, :w], func=ACT.Sigmoid)
+        def act_chunk(t, c):
+            if c == 0:
+                gates[t] = work.tile([P, NG], F32, name="gates", bufs=3, align_bytes=64)
+                nc.scalar.activation(out=gate(t, 0, 2), in_=pre[t, c][:], func=ACT.Sigmoid)
+            elif c == 1:
+                nc.scalar.activation(out=gate(t, 2), in_=pre[t, c][:, DH:], func=ACT.Tanh)
+                nc.scalar.activation(out=gate(t, 3), in_=pre[t, c][:, :DH], func=ACT.Sigmoid)
+            else:
+                nc.scalar.activation(out=gate(t, c + 2, c - 1), in_=pre[t, c][:], func=ACT.Sigmoid)
 
         def act_tanh_c(t):
             tanh_c[t] = work.tile([P, DH], F32, name="tanh_c", align_bytes=64)
@@ -274,109 +333,192 @@ def tile_share_lstm_cell_pa_kernel(
                 elif t % 2 == 1:
                     nc.sync.dma_start(out=rows(out_of_slot[n])[:, t - 1 : t + 1, :], in_=outs[t // 2][:, n, :, :])
 
-        def weight_transposes(tag, wt, c, block, count, engine):
-            ps = psum.tile([P, count, P], BF16, name="wt_ps", tag=tag)
+        def weight_transposes(tag, wt, e, block, count, engine):
+            ps = psum.tile([P, count, P], BF16, name="wt_ps", tag=tag, bufs=(3 if tag == "rot" else 1))
             for j in range(count):
-                nc.tensor.matmul(ps[:, j, :], lhsT=block(j)[:, P * c : P * (c + 1)], rhs=ident_b[:], start=True, stop=True)
-            copy_on(engine, wt[:, c, :], ps[:].rearrange("p j n -> p (j n)"))
+                nc.tensor.matmul(ps[:, j, :], lhsT=block(j)[:, e :: 2], rhs=ident_b[:], start=True, stop=True)
+            copy_on(engine, wt[:, e, :], ps[:].rearrange("p j n -> p (j n)"))
 
-        def bias_transpose(half):
-            ps = psum.tile([P, P], BF16, name="bias_ps", tag="tr", bufs=2)
-            nc.tensor.transpose(ps[:], bias_rows[:, half, :], ident_b[:])
-            if half == 0:
-                nc.vector.tensor_copy(out=bias_two[:], in_=ps[:, 0:32])
-                nc.vector.tensor_tensor(out=bias_hh_col[:], in0=bias_two[:, 0:HH_BLOCKS],
-                                        in1=bias_two[:, OTHER_BIAS_ROW : OTHER_BIAS_ROW + HH_BLOCKS], op=ALU.add)
-            else:
-                nc.vector.tensor_tensor(out=bias_s_col[:], in0=ps[:, 0 : BLOCKS - HH_BLOCKS],
-                                        in1=bias_two[:, HH_BLOCKS:BLOCKS], op=ALU.add)
-
-        for t, engine in ((0, "dve"), (1, "act")):
+        def x_transposes(t):
             for i in range(4):
                 x_transpose(t, i)
-            x_copy(t, engine)
-        bias_transpose(0)
+
+        def bias_broadcast(c):
+            c0, c1 = CHUNKS[c]
+            ps = psum.tile([P, c1 - c0], F32, name="bias_ps", tag="rot", bufs=3)
+            nc.tensor.matmul(ps[:], lhsT=ones[:], rhs=bias_rows[:, c0:c1], start=True, stop=True)
+            nc.scalar.copy(out=bias_all[:, c0:c1], in_=ps[:])
+
+        def bias_columns():
+            ps = psum.tile([P, T_BLOCKS, 2], F32, name="bias_col_ps", tag="rot", bufs=3)
+            for j in range(T_BLOCKS):
+                nc.tensor.matmul(ps[:, j, :], lhsT=bias_rows[:, P * j : P * (j + 1)], rhs=ones[:, 0:2], start=True, stop=True)
+            nc.scalar.copy(out=bias_hh_col[:], in_=ps[:, :, 0])
+
+        def wsh_block(j):
+            return wsh_raw[j // 2][:, j % 2, :]
+
+        def steps(names, t):
+            for name in names:
+                step(name, t)
+
+        def nothing():
+            return None
+
+        x_transposes(0)
+        x_copy(0, "dve")
         quantize(0)
-        for c in range(2):
-            weight_transposes(("gA", "gB")[c], wt_hh, c, lambda j: whh_raw[:, j, :], HH_BLOCKS, "act")
-        mx_pair(0, HH_PAIRS[0])
-        mx_copy(0, HH_PAIRS[0], "dve")
-        for i in range(8):
-            hs_transpose(0, i)
-        hs_copy(0, "act")
-        mx_pair(0, HH_PAIRS[1])
-        mx_copy(0, HH_PAIRS[1], "dve")
-        bias_transpose(1)
+        weight_transposes("gA", wt_hh, 0, lambda j: whh_raw[:, j, :], HH_BLOCKS, "act")
+        hs_transposes(0, 0, 1)
+        hs_copy(0, "dve", 0, 1)
+        weight_transposes("gB", wt_hh, 1, lambda j: whh_raw[:, j, :], HH_BLOCKS, "dve")
+        bias_broadcast(0)
+        bias_broadcast(1)
         for m, factor in ((m1, 1.0), (m2, 0.5), (m3, 1.0 / 3.0)):
             nc.vector.tensor_scalar(out=m[:], in0=mask_sb[:], scalar1=factor, scalar2=None, op0=ALU.mult)
 
-        all_pairs = [(s, pair) for s in range(TILES // 2) for pair in HH_PAIRS + S_PAIRS]
-        done = 2
-        for t in range(TILES):
+        chunk_products(0, 0, ("sX", "sP"), nothing)
+        chunk_products(0, 1, ("gA", "gB"), nothing)
+        chunk_sum("p", 0, 0)
+        chunk_sum("p", 0, 1)
+        chunk_sum("q", 0, 0)
+        chunk_sum("q", 0, 1)
+        act_chunk(0, 0)
+        x_transposes(1)
+        x_copy(1, "dve")
+        hs_transposes(0, 1, 4)
+        hs_copy(0, "act", 1, 4)
+        act_chunk(0, 1)
+        for e in range(2):
+            weight_transposes("rot", wt_s, e, wsh_block, 6, ("act", "dve")[e])
+        bias_broadcast(2)
+        chunk_products(0, 2, ("gC",), nothing)
+        bias_broadcast(3)
+        hs_transposes(1)
+        hs_copy(1, "act")
+        chunk_products(0, 3, ("sX", "sP"), nothing)
+        chunk_sum("p", 0, 2)
+        quantize(1)
+        chunk_sum("q", 0, 2)
+        act_chunk(0, 2)
+        step("fc", 0)
+        chunk_sum("p", 0, 3)
+        step("ig", 0)
+        chunk_sum("q", 0, 3)
+        step("ct", 0)
+        act_chunk(0, 3)
+        act_tanh_c(0)
+        chunk_products(1, 0, ("gA", "gB"), nothing)
+        for xt in (2, 3):
+            x_transposes(xt)
+            x_copy(xt, "act")
+        chunk_products(1, 1, ("sX", "sP"), nothing)
+        bias_columns()
+        chunk_sum("p", 1, 0)
+        step("d0", 0)
+        chunk_sum("q", 1, 0)
+        act_chunk(1, 0)
+        step("d1", 0)
+        chunk_sum("p", 1, 1)
+        quantize(2)
+        chunk_sum("q", 1, 1)
+        act_chunk(1, 1)
+        hs_transposes(2)
+        hs_copy(2, "act")
+        chunk_products(1, 2, ("gC",), lambda: mx_pair(1, PAIRS[0]))
+        mx_copy(1, PAIRS[0], "act")
+        chunk_products(1, 3, ("gA", "gB"), lambda: mx_pair(1, PAIRS[1]))
+        mx_copy(1, PAIRS[1], "act")
+        steps(("hs0", "d2", "e1", "f2", "s1"), 0)
+        chunk_sum("p", 1, 2)
+        step("e2", 0)
+        chunk_sum("q", 1, 2)
+        act_chunk(1, 2)
+        step("s2", 0)
+        x_transposes(4)
+        x_copy(4, "act")
+        mx_pair(1, PAIRS[2])
+        mx_copy(1, PAIRS[2], "act")
+        chunk_sum("p", 1, 3)
+        steps(("fc", "ig"), 1)
+        chunk_sum("q", 1, 3)
+        step("ct", 1)
+        store(1, (0,))
+        act_chunk(1, 3)
+        act_tanh_c(1)
+
+        for t in range(2, TILES - 1):
+            s, odd = divmod(t, 2)
             r = t - 1
-            slots = PAIR_SLOTS[t]
-            pairs = dict(zip(slots, all_pairs[done : done + len(slots)]))
-            done += len(slots)
-            if r >= 0:
-                step("d0", r)
-                step("d1", r)
-            for k, j in enumerate(BLOCK_ORDER):
-                gate_group(t, j, (lambda a=pairs.get(k): mx_pair(*a) if a else None))
-                if k == 0 and r >= 0:
-                    act_tanh_c(r)
-                    for name in ("hs0", "d2"):
-                        step(name, r)
-                    if t in (2, 3):
-                        quantize(t)
-                    for name in ("e1", "f2", "s1"):
-                        step(name, r)
-                    store(r, (0, 1, 2, 3))
-                if k == 6:
-                    act_if(t)
-                if k == 12:
-                    act_shared(t, 0)
-                if k in pairs:
-                    mx_copy(*pairs[k], "dve" if t == 0 else "act")
-                if t == 0:
-                    if k in (1, 3):
-                        weight_transposes(("gC", "gD")[k // 2], wt_s, k // 2, lambda j: wsh_raw[j // 2][:, j % 2, :], 6, "dve")
-                    if 2 <= k < 10:
-                        x_transpose(2 + (k - 2) // 4, (k - 2) % 4)
-                    if k in (5, 9):
-                        x_copy(2 + k // 9, "dve")
-                    if k == 9:
-                        quantize(1)
-                if t + 1 < TILES and k < 4:
-                    hs_transpose(t + 1, 2 * k)
-                    hs_transpose(t + 1, 2 * k + 1)
-                    if k == 3:
-                        hs_copy(t + 1, "act")
-                if t in (1, 2) and 4 <= k < 12:
-                    x_transpose(2 * t + 2 + (k - 4) // 4, k % 4)
-                    if k == 7:
-                        x_copy(2 * t + 2, "dve")
-                if k == 7:
-                    act_go(t)
-                if k == (9 if t == 0 else 7):
-                    step("fc", t)
-                    if r >= 0:
-                        step("e2", r)
-                    step("ig", t)
-                    if r >= 0:
-                        step("s2", r)
-                        store(r, (4,))
-                    step("ct", t)
-                if k == 11 and t in (1, 2):
-                    x_copy(2 * t + 3, "dve")
-                if k == 13:
-                    act_shared(t, 1)
-        r = TILES - 1
-        act_tanh_c(r)
-        store(r, (0,))
-        for name in ("d0", "d1", "hs0", "d2", "e1", "f2", "s1", "e2", "s2"):
-            step(name, r)
-            if name == "hs0":
-                store(r, (1, 2))
-            if name == "s1":
-                store(r, (3,))
+            if not odd:
+                later = {-1: (s, PAIRS[3]), 1: (s, PAIRS[4])}
+            elif t + 1 < TILES:
+                later = {0: (s + 1, PAIRS[0]), 2: (s + 1, PAIRS[1]), 3: (s + 1, PAIRS[2])}
+            else:
+                later = {}
+            chunk_products(t, 3, ("sX", "sP"), (lambda a=later.get(-1): mx_pair(*a) if a else None))
+            if -1 in later:
+                mx_copy(*later[-1], "act")
+            steps(("d0", "d1", "d2", "hs0"), r)
+            chunk_sum("p", t, 3)
+            steps(("e1", "f2", "s1"), r)
+            store(r, (1, 2, 3))
+            chunk_sum("q", t, 3)
+            step("e2", r)
+            for q in range(4):
+                if q == 0 and t + 1 < TILES:
+                    hs_transposes(t + 1)
+                    hs_copy(t + 1, "act")
+                if q == 2 and t + 3 < TILES:
+                    x_transposes(t + 3)
+                    x_copy(t + 3, "act")
+                gate_round(t, q, (lambda a=later.get(q): mx_pair(*a) if a else None))
+                if q in later and q < 3:
+                    mx_copy(*later[q], "act")
+            if not odd and t < TILES - 2:
+                quantize(t + 2)
+            act_first(t)
+            for q in range(2):
+                o_group(t, q)
+            steps(("ig", "fc"), t)
+            step("s2", r)
+            store(r, (4,))
+            step("ct", t)
+            store(t, (0,))
+            act_chunk(t, 3)
+            act_o(t)
+            if 3 in later:
+                mx_copy(*later[3], "act")
+            act_tanh_c(t)
+        t, r = TILES - 1, TILES - 2
+        chunk_products(t, 3, ("sX", "sP"), nothing)
+        for q in range(4):
+            gate_round(t, q, nothing)
+        steps(("d0", "d1", "d2"), r)
+        chunk_sum("p", t, 3)
+        step("hs0", r)
+        store(r, (1, 2))
+        chunk_sum("q", t, 3)
+        act_first(t)
+        for q in range(2):
+            o_group(t, q)
+        act_o(t)
+        act_chunk(t, 3)
+        steps(("ig", "fc"), t)
+        step("e1", r)
+        step("ct", t)
+        store(t, (0,))
+        act_tanh_c(t)
+        step("f2", r)
+        steps(("d0", "d1", "d2", "hs0"), t)
+        store(t, (1, 2))
+        step("s1", r)
+        store(r, (3,))
+        step("e1", t)
+        step("e2", r)
+        steps(("f2", "s1"), t)
+        store(t, (3,))
+        step("s2", r)
         store(r, (4,))
+        steps(("e2", "s2"), t)
+        store(t, (4,))

@@ -21,8 +21,8 @@ P = 128
 TILES = B // P
 PASSES = DI // 512
 HH_BLOCKS = 4 * DH // P
-PAIR_ROWS = 2 * P
-PAIRS = [(0, 2), (1, 3), (6, 8), (7, 9), (4, 5)]
+PAIRS = [(0, 2), (1, 3), (6, 8), (7, 9), (4, 5), (10, 12), (11, 13)]
+UNITS = [(0, 1), (1, 2), (3, 2), (5, 2), (7, 1)]
 T_BLOCKS = 10
 T_COLS = T_BLOCKS * P
 A_COLS = NG - T_COLS
@@ -77,9 +77,6 @@ def tile_share_lstm_cell_pa_kernel(
         nc.vector.memset(bias_rows[:].bitcast(I32), 0)
         nc.vector.memset(ones[:], 1.0)
         nc.vector.tensor_copy(out=ident_b[:], in_=ident_f[:])
-        for i, vec in enumerate((bias_sh0, bias_sh1, bias_sh2)):
-            nc.gpsimd.dma_start(out=bias_rows[1:2, DH * (4 + i) : DH * (5 + i)], in_=vec.rearrange("(a n) -> a n", a=1))
-        nc.gpsimd.dma_start(out=mask_sb[:], in_=mask.rearrange("(p t) -> p t", t=TILES))
 
         states = (("h", h_minors), ("s0", s0), ("s1", s1), ("s2", s2))
         load_x(0, 1)
@@ -92,9 +89,11 @@ def tile_share_lstm_cell_pa_kernel(
                 out=plane[32 * q : 32 * q + 4, :, :].bitcast(I32),
                 in_=weight_ih_scales[:, 4 * q : 4 * q + 4, :].rearrange("g r n -> r g n").bitcast(I32),
             )
-        nc.scalar.dma_start(out=bias_rows[0:1, :], in_=bias_ih.rearrange("(a n) -> a n", a=1))
-        nc.scalar.dma_start(out=bias_rows[1:2, : 4 * DH], in_=bias_hh.rearrange("(a n) -> a n", a=1))
-        load_x(1, 1)
+        nc.sync.dma_start(out=bias_rows[0:1, :], in_=bias_ih.rearrange("(a n) -> a n", a=1))
+        nc.sync.dma_start(out=bias_rows[1:2, : 4 * DH], in_=bias_hh.rearrange("(a n) -> a n", a=1))
+        load_x(1, 2)
+        for i, vec in enumerate((bias_sh0, bias_sh1, bias_sh2)):
+            nc.sync.dma_start(out=bias_rows[1:2, DH * (4 + i) : DH * (5 + i)], in_=vec.rearrange("(a n) -> a n", a=1))
         for key, src in states[1:]:
             load_state(key, src, 0, 2)
         wsh_raw = []
@@ -102,25 +101,25 @@ def tile_share_lstm_cell_pa_kernel(
             wr = keep.tile([P, 2, DH], BF16, name="wsh_raw%d" % i, align_bytes=64)
             nc.sync.dma_start(out=wr[:], in_=w.rearrange("(j p) k -> p j k", p=P))
             wsh_raw.append(wr)
-        words_s = load_words("words_s", T_COLS, NG)
+        nc.sync.dma_start(out=mask_sb[:], in_=mask.rearrange("(p t) -> p t", t=TILES))
         load_state("c", c_minors, 0, 2)
-        load_x(2, 2)
+        words_s = load_words("words_s", T_COLS, NG)
+        load_x(3, 2)
         for key, src in states:
             load_state(key, src, 2, TILES - 2)
-        load_x(4, 2)
         load_state("c", c_minors, 2, TILES - 2)
-        load_x(6, 2)
+        load_x(5, 3)
 
         wt_hh = keep.tile([P, 2, 4 * DH], BF16, name="wt_hh", align_bytes=64)
         wt_s = keep.tile([P, 2, 3 * DH], BF16, name="wt_s", align_bytes=64)
-        bias_hh_col = keep.tile([P, T_BLOCKS], F32, name="bias_hh_col")
+        bias_hh_col = keep.tile([P, NG // P], F32, name="bias_hh_col")
         bias_all = keep.tile([P, NG], F32, name="bias_all", align_bytes=64)
         m1 = keep.tile([P, TILES], F32, name="m1")
         m2 = keep.tile([P, TILES], F32, name="m2")
         m3 = keep.tile([P, TILES], F32, name="m3")
 
         grouped, codes, scales, mx_sb, hs_t, gates, tanh_c, outs, banks = {}, {}, {}, {}, {}, {}, {}, {}, {}
-        xt_ps, hs_ps, mx_ps, pre = {}, {}, {}, {}
+        xt_ps, hs_ps, mx_ps, pre, x_sorted = {}, {}, {}, {}, {}
 
         def copy_on(engine, out, in_):
             if engine == "act":
@@ -128,15 +127,20 @@ def tile_share_lstm_cell_pa_kernel(
             else:
                 nc.vector.tensor_copy(out=out, in_=in_)
 
+        def x_sort(t):
+            x_sorted[t] = work.tile([P, PASSES, 2, P], F32, name="x_sorted", bufs=3, align_bytes=64)
+            words = x_sb[t].bitcast(F32).rearrange("r (g p u) -> r g u p", g=PASSES, u=2)
+            nc.vector.tensor_copy(out=x_sorted[t][:], in_=words)
+
         def x_transpose(t, i):
             g, u = divmod(i, 2)
             if i == 0:
                 xt_ps[t] = psum.tile([P, PASSES, 2, P], F32, name="xt_ps", tag="rot", bufs=3)
-            words = x_sb[t].bitcast(F32)
-            nc.tensor.transpose(xt_ps[t][:, g, u, :], words[:, 256 * g + u : 256 * (g + 1) : 2], ident_f[:])
+            nc.tensor.transpose(xt_ps[t][:, g, u, :], x_sorted[t][:, g, u, :], ident_f[:])
 
         def unit_of(t):
-            return ((t, 1), 0) if t < 2 else ((t - t % 2, 2), t % 2)
+            unit = UNITS[(t + 1) // 2]
+            return unit, t - unit[0]
 
         def x_copy(t, engine):
             unit, tt = unit_of(t)
@@ -168,22 +172,23 @@ def tile_share_lstm_cell_pa_kernel(
             return hs_t[t][:, i, :].bitcast(BF16)[:, e :: 2]
 
         def mx_pair(s, pair):
-            ps = psum.tile([P, 2, PAIR_ROWS], F32, name="mx_ps", tag="rot", bufs=3)
+            ps = psum.tile([P, 2, s[1] * P], F32, name="mx_ps", tag="rot", bufs=3)
             mx_ps[s, pair] = ps
             for i, j in enumerate(pair):
+                words, jj = (words_hh, j) if j < T_BLOCKS else (words_s, j - T_BLOCKS)
                 for g in range(PASSES):
                     nc.tensor.matmul_mx(
                         out=ps[:, i, :],
-                        lhsT=words_hh[:, g, 2 * P * j : 2 * P * (j + 1)].bitcast(E2M1X4),
+                        lhsT=words[:, g, 2 * P * jj : 2 * P * (jj + 1)].bitcast(E2M1X4),
                         lhsT_scale=plane[:, g, P * j : P * (j + 1)],
-                        rhs=codes[2 * s, 2][:, g, :].bitcast(E5M2X4),
-                        rhs_scale=scales[2 * s, 2][:, g, :],
+                        rhs=codes[s][:, g, :].bitcast(E5M2X4),
+                        rhs_scale=scales[s][:, g, :],
                         start=(g == 0),
                         stop=(g == PASSES - 1),
                     )
 
         def mx_copy(s, pair, engine):
-            sb = work.tile([P, 2, PAIR_ROWS], F32, name="mx_sb", bufs=10, align_bytes=64)
+            sb = work.tile([P, 2, s[1] * P], F32, name="mx_sb", bufs=12, align_bytes=64)
             ps = mx_ps[s, pair]
             j0, j1 = pair
             for i, j in enumerate(pair):
@@ -192,23 +197,24 @@ def tile_share_lstm_cell_pa_kernel(
                 for i, j in enumerate(pair):
                     nc.scalar.activation(out=sb[:, i, :], in_=ps[:, i, :], func=ACT.Identity, bias=bias_hh_col[:, j : j + 1])
             else:
-                both = bias_hh_col[:, j0 : j1 + 1 : j1 - j0].unsqueeze(2).to_broadcast([P, 2, PAIR_ROWS])
+                both = bias_hh_col[:, j0 : j1 + 1 : j1 - j0].unsqueeze(2).to_broadcast([P, 2, s[1] * P])
                 nc.vector.tensor_tensor(out=sb[:], in0=ps[:], in1=both, op=ALU.add)
 
         def open_group(t, j, tag, q):
-            s, tt = divmod(t, 2)
+            s, tt = unit_of(t)
             if q == 0:
                 banks[t, tag] = psum.tile([P, 4 * P], F32, name=tag, tag=tag)
             nc.tensor.matmul(banks[t, tag][:, P * q : P * (q + 1)], lhsT=mx_sb[s, j][:, P * tt : P * (tt + 1)],
                              rhs=ident_f[:], is_transpose=True, start=True, stop=False)
 
         def plain_pass(t, j, tag, q, e):
-            state, wt, jj = (0, wt_hh, j) if j < HH_BLOCKS else (1, wt_s, j - HH_BLOCKS)
+            state, wt, jj = (0, wt_hh, j) if j < HH_BLOCKS else (j // 2 - 3, wt_s, j - HH_BLOCKS)
             nc.tensor.matmul(banks[t, tag][:, P * q : P * (q + 1)], lhsT=state_t(t, state, e),
                              rhs=wt[:, e, P * jj : P * (jj + 1)], start=False, stop=(e == 1))
 
-        def gate_round(t, q, between):
-            blocks = list(zip(PAIRS[q], ("gA", "gB")))
+        def gate_round(t, n, between):
+            q, tags = (n, ("gA", "gB")) if n < 4 else (n - 5, ("sX", "sP"))
+            blocks = list(zip(PAIRS[n], tags))
             for j, tag in blocks:
                 open_group(t, j, tag, q)
             for e in range(2):
@@ -312,6 +318,10 @@ def tile_share_lstm_cell_pa_kernel(
                 th = tanh_c[t][:].unsqueeze(1).to_broadcast([P, 2, DH])
                 stt(outs[t // 2][:, 1:3, t % 2, :], th, m1[:, col],
                     gate(t, 3, 2).rearrange("p (a d) -> p a d", a=2), ALU.mult, ALU.mult)
+            elif name == "h":
+                stt(out_slot(t, 1), tanh_c[t][:], m1[:, col], gate(t, 3), ALU.mult, ALU.mult)
+            elif name == "s0":
+                stt(out_slot(t, 2), tanh_c[t][:], m1[:, col], gate(t, 4), ALU.mult, ALU.mult)
             elif name == "e1":
                 nc.vector.tensor_tensor(out=gate(t, 5), in0=gate(t, 5), in1=out_slot(t, 2), op=ALU.subtract)
             elif name == "f2":
@@ -350,8 +360,8 @@ def tile_share_lstm_cell_pa_kernel(
             nc.scalar.copy(out=bias_all[:, c0:c1], in_=ps[:])
 
         def bias_columns():
-            ps = psum.tile([P, T_BLOCKS, 2], F32, name="bias_col_ps", tag="rot", bufs=3)
-            for j in range(T_BLOCKS):
+            ps = psum.tile([P, NG // P, 2], F32, name="bias_col_ps", tag="rot", bufs=3)
+            for j in range(NG // P):
                 nc.tensor.matmul(ps[:, j, :], lhsT=bias_rows[:, P * j : P * (j + 1)], rhs=ones[:, 0:2], start=True, stop=True)
             nc.scalar.copy(out=bias_hh_col[:], in_=ps[:, :, 0])
 
@@ -365,6 +375,7 @@ def tile_share_lstm_cell_pa_kernel(
         def nothing():
             return None
 
+        x_sort(0)
         x_transposes(0)
         x_copy(0, "dve")
         quantize(0)
@@ -374,8 +385,8 @@ def tile_share_lstm_cell_pa_kernel(
         weight_transposes("gB", wt_hh, 1, lambda j: whh_raw[:, j, :], HH_BLOCKS, "dve")
         bias_broadcast(0)
         bias_broadcast(1)
-        for m, factor in ((m1, 1.0), (m2, 0.5), (m3, 1.0 / 3.0)):
-            nc.vector.tensor_scalar(out=m[:], in0=mask_sb[:], scalar1=factor, scalar2=None, op0=ALU.mult)
+        x_sort(1)
+        x_sort(2)
 
         chunk_products(0, 0, ("sX", "sP"), nothing)
         chunk_products(0, 1, ("gA", "gB"), nothing)
@@ -386,97 +397,81 @@ def tile_share_lstm_cell_pa_kernel(
         act_chunk(0, 0)
         x_transposes(1)
         x_copy(1, "dve")
+        x_transposes(2)
+        x_copy(2, "act")
         hs_transposes(0, 1, 4)
-        hs_copy(0, "act", 1, 4)
         act_chunk(0, 1)
-        for e in range(2):
-            weight_transposes("rot", wt_s, e, wsh_block, 6, ("act", "dve")[e])
+        hs_copy(0, "act", 1, 4)
+        quantize(1)
+        for m, factor in ((m1, 1.0), (m2, 0.5), (m3, 1.0 / 3.0)):
+            nc.vector.tensor_scalar(out=m[:], in0=mask_sb[:], scalar1=factor, scalar2=None, op0=ALU.mult)
+        weight_transposes("sX", wt_s, 0, wsh_block, 6, "act")
+        weight_transposes("sP", wt_s, 1, wsh_block, 6, "dve")
         bias_broadcast(2)
-        chunk_products(0, 2, ("gC",), nothing)
+        bias_columns()
+        steps(("fc", "ig"), 0)
+        x_sort(3)
+        chunk_products(0, 2, ("gC",), lambda: mx_pair(UNITS[1], PAIRS[0]))
         bias_broadcast(3)
+        chunk_sum("p", 0, 2)
+        step("ct", 0)
+        mx_copy(UNITS[1], PAIRS[0], "dve")
+        chunk_sum("q", 0, 2)
+        act_tanh_c(0)
         hs_transposes(1)
         hs_copy(1, "act")
-        chunk_products(0, 3, ("sX", "sP"), nothing)
-        chunk_sum("p", 0, 2)
-        quantize(1)
-        chunk_sum("q", 0, 2)
         act_chunk(0, 2)
-        step("fc", 0)
+        chunk_products(0, 3, ("gA", "gB"), lambda: mx_pair(UNITS[1], PAIRS[1]))
         chunk_sum("p", 0, 3)
-        step("ig", 0)
-        chunk_sum("q", 0, 3)
-        step("ct", 0)
-        act_chunk(0, 3)
-        act_tanh_c(0)
-        chunk_products(1, 0, ("gA", "gB"), nothing)
-        for xt in (2, 3):
-            x_transposes(xt)
-            x_copy(xt, "act")
-        chunk_products(1, 1, ("sX", "sP"), nothing)
-        bias_columns()
-        chunk_sum("p", 1, 0)
+        mx_copy(UNITS[1], PAIRS[1], "act")
         step("d0", 0)
-        chunk_sum("q", 1, 0)
-        act_chunk(1, 0)
-        step("d1", 0)
-        chunk_sum("p", 1, 1)
-        quantize(2)
-        chunk_sum("q", 1, 1)
-        act_chunk(1, 1)
-        hs_transposes(2)
-        hs_copy(2, "act")
-        chunk_products(1, 2, ("gC",), lambda: mx_pair(1, PAIRS[0]))
-        mx_copy(1, PAIRS[0], "act")
-        chunk_products(1, 3, ("gA", "gB"), lambda: mx_pair(1, PAIRS[1]))
-        mx_copy(1, PAIRS[1], "act")
-        steps(("hs0", "d2", "e1", "f2", "s1"), 0)
-        chunk_sum("p", 1, 2)
-        step("e2", 0)
-        chunk_sum("q", 1, 2)
-        act_chunk(1, 2)
-        step("s2", 0)
-        x_transposes(4)
-        x_copy(4, "act")
-        mx_pair(1, PAIRS[2])
-        mx_copy(1, PAIRS[2], "act")
-        chunk_sum("p", 1, 3)
-        steps(("fc", "ig"), 1)
-        chunk_sum("q", 1, 3)
-        step("ct", 1)
-        store(1, (0,))
-        act_chunk(1, 3)
-        act_tanh_c(1)
+        chunk_sum("q", 0, 3)
+        x_transposes(3)
+        mx_pair(UNITS[1], PAIRS[2])
+        act_chunk(0, 3)
+        x_copy(3, "dve")
+        mx_copy(UNITS[1], PAIRS[2], "act")
 
-        for t in range(2, TILES - 1):
-            s, odd = divmod(t, 2)
+        for t in range(1, TILES - 1):
+            unit, follows = unit_of(t)
             r = t - 1
-            if not odd:
-                later = {-1: (s, PAIRS[3]), 1: (s, PAIRS[4])}
-            elif t + 1 < TILES:
-                later = {0: (s + 1, PAIRS[0]), 2: (s + 1, PAIRS[1]), 3: (s + 1, PAIRS[2])}
+            if not follows:
+                later = {-1: [(unit, PAIRS[3])], 1: [(unit, PAIRS[4])]}
+            elif t + 2 < TILES:
+                later = {q: [(unit_of(t + 1)[0], PAIRS[n])] for n, q in enumerate((0, 2, 3))}
             else:
-                later = {}
-            chunk_products(t, 3, ("sX", "sP"), (lambda a=later.get(-1): mx_pair(*a) if a else None))
-            if -1 in later:
-                mx_copy(*later[-1], "act")
-            steps(("d0", "d1", "d2", "hs0"), r)
+                later = {q: [(unit_of(t + 1)[0], PAIRS[n])] for n, q in enumerate((-1, 0, 1, 2, 3))}
+
+            def pairs_at(q, later=later):
+                for a in later.get(q, []):
+                    mx_pair(*a)
+
+            def copies_at(q, later=later):
+                for a in later.get(q, []):
+                    mx_copy(*a, "act")
+
+            chunk_products(t, 3, ("sX", "sP"), lambda: pairs_at(-1))
+            copies_at(-1)
+            if t + 3 < TILES:
+                x_sort(t + 3)
+            steps(("hs0", "d1", "d2") if t == 1 else ("d0", "d1", "d2", "hs0"), r)
             chunk_sum("p", t, 3)
             steps(("e1", "f2", "s1"), r)
             store(r, (1, 2, 3))
             chunk_sum("q", t, 3)
             step("e2", r)
             for q in range(4):
-                if q == 0 and t + 1 < TILES:
+                if q == 0:
                     hs_transposes(t + 1)
                     hs_copy(t + 1, "act")
                 if q == 2 and t + 3 < TILES:
                     x_transposes(t + 3)
                     x_copy(t + 3, "act")
-                gate_round(t, q, (lambda a=later.get(q): mx_pair(*a) if a else None))
-                if q in later and q < 3:
-                    mx_copy(*later[q], "act")
-            if not odd and t < TILES - 2:
-                quantize(t + 2)
+                gate_round(t, q, lambda: pairs_at(q))
+                if q < 3:
+                    copies_at(q)
+            if t in (1, 3, 4):
+                quantize(t + 3 - t % 2)
             act_first(t)
             for q in range(2):
                 o_group(t, q)
@@ -487,38 +482,39 @@ def tile_share_lstm_cell_pa_kernel(
             store(t, (0,))
             act_chunk(t, 3)
             act_o(t)
-            if 3 in later:
-                mx_copy(*later[3], "act")
+            copies_at(3)
             act_tanh_c(t)
         t, r = TILES - 1, TILES - 2
-        chunk_products(t, 3, ("sX", "sP"), nothing)
+        for n in (5, 6):
+            mx_pair(UNITS[-1], PAIRS[n])
+            mx_copy(UNITS[-1], PAIRS[n], "act")
         for q in range(4):
             gate_round(t, q, nothing)
-        steps(("d0", "d1", "d2"), r)
-        chunk_sum("p", t, 3)
-        step("hs0", r)
-        store(r, (1, 2))
-        chunk_sum("q", t, 3)
-        act_first(t)
+        steps(("d0", "d1", "hs0", "d2", "e1", "f2", "s1"), r)
+        store(r, (1, 2, 3))
+        gates[t] = work.tile([P, NG], F32, name="gates", bufs=3, align_bytes=64)
+        nc.scalar.activation(out=gate(t, 1), in_=banks[t, "gB"][:, :DH], func=ACT.Sigmoid)
+        nc.scalar.activation(out=gate(t, 0), in_=banks[t, "gA"][:, :DH], func=ACT.Sigmoid)
+        nc.scalar.activation(out=gate(t, 2), in_=banks[t, "gA"][:, DH:], func=ACT.Tanh)
+        nc.scalar.activation(out=gate(t, 4), in_=banks[t, "gB"][:, DH:], func=ACT.Sigmoid)
         for q in range(2):
             o_group(t, q)
+        for q in range(2):
+            gate_round(t, 5 + q, nothing)
         act_o(t)
-        act_chunk(t, 3)
-        steps(("ig", "fc"), t)
-        step("e1", r)
+        step("fc", t)
+        step("e2", r)
+        step("ig", t)
+        step("s2", r)
+        store(r, (4,))
         step("ct", t)
         store(t, (0,))
         act_tanh_c(t)
-        step("f2", r)
-        steps(("d0", "d1", "d2", "hs0"), t)
-        store(t, (1, 2))
-        step("s1", r)
-        store(r, (3,))
-        step("e1", t)
-        step("e2", r)
-        steps(("f2", "s1"), t)
-        store(t, (3,))
-        step("s2", r)
-        store(r, (4,))
-        steps(("e2", "s2"), t)
+        for n, tag in ((5, "sX"), (6, "sP")):
+            nc.scalar.activation(out=gate(t, n), in_=banks[t, tag][:, :DH], func=ACT.Sigmoid)
+        steps(("d0", "s0", "d1", "d2", "e1", "f2", "s1"), t)
+        store(t, (2, 3))
+        steps(("h", "e2"), t)
+        store(t, (1,))
+        step("s2", t)
         store(t, (4,))

@@ -22,6 +22,7 @@ TILES = B // P
 PASSES = DI // 512
 HH_BLOCKS = 4 * DH // P
 PAIRS = [(0, 2), (1, 3), (6, 8), (7, 9), (4, 5), (10, 12), (11, 13)]
+P_ENGINE = ("act", "dve", "act")
 UNITS = [(0, 1), (1, 2), (3, 2), (5, 2), (7, 1)]
 T_BLOCKS = 10
 T_COLS = T_BLOCKS * P
@@ -113,7 +114,7 @@ def tile_share_lstm_cell_pa_kernel(
         wt_hh = keep.tile([P, 2, 4 * DH], BF16, name="wt_hh", align_bytes=64)
         wt_s = keep.tile([P, 2, 3 * DH], BF16, name="wt_s", align_bytes=64)
         bias_hh_col = keep.tile([P, NG // P], F32, name="bias_hh_col")
-        bias_all = keep.tile([P, NG], F32, name="bias_all", align_bytes=64)
+        bias_all = keep.tile([P, A_COLS], F32, name="bias_all", align_bytes=64)
         m1 = keep.tile([P, TILES], F32, name="m1")
         m2 = keep.tile([P, TILES], F32, name="m2")
         m3 = keep.tile([P, TILES], F32, name="m3")
@@ -161,7 +162,13 @@ def tile_share_lstm_cell_pa_kernel(
         def hs_transposes(t, first=0, last=4):
             hs_ps[t] = psum.tile([P, 4, P], F32, name="hs_ps", tag="rot", bufs=3)
             for i in range(first, last):
-                nc.tensor.transpose(hs_ps[t][:, i, :], state_sb[states[i][0], t].bitcast(F32), ident_f[:])
+                src = state_sb[states[i][0], t]
+                if i == 0:
+                    for e in range(2):
+                        cols = slice(P * e, P * (e + 1))
+                        nc.tensor.transpose(hs_ps[t][:, i, :].bitcast(BF16)[:, cols], src[:, cols], ident_b[:])
+                else:
+                    nc.tensor.transpose(hs_ps[t][:, i, :], src.bitcast(F32), ident_f[:])
 
         def hs_copy(t, engine, first=0, last=4):
             if first == 0:
@@ -169,7 +176,8 @@ def tile_share_lstm_cell_pa_kernel(
             copy_on(engine, hs_t[t][:, first:last, :], hs_ps[t][:, first:last, :])
 
         def state_t(t, i, e):
-            return hs_t[t][:, i, :].bitcast(BF16)[:, e :: 2]
+            values = hs_t[t][:, i, :].bitcast(BF16)
+            return values[:, P * e : P * (e + 1)] if i == 0 else values[:, e :: 2]
 
         def mx_pair(s, pair):
             ps = psum.tile([P, 2, s[1] * P], F32, name="mx_ps", tag="rot", bufs=3)
@@ -255,16 +263,22 @@ def tile_share_lstm_cell_pa_kernel(
                 parts = [(0, wt_hh, c0, c1, 0)]
             else:
                 parts = [(n - 3, wt_s, DH * (n - 4), DH * (n - 3), DH * n - c0) for n in range(c0 // DH, c1 // DH)]
+            bias_first = c < 3
+            if bias_first:
+                nc.tensor.matmul(plain_out, lhsT=ones[:], rhs=bias_rows[:, c0:c1], start=True, stop=False)
             for state, wt, w0, w1, o0 in parts:
                 for e in range(2):
                     nc.tensor.matmul(plain_out[:, o0 : o0 + w1 - w0], lhsT=state_t(t, state, e), rhs=wt[:, e, w0:w1],
-                                     start=(e == 0), stop=(e == 1))
+                                     start=(e == 0 and not bias_first), stop=(e == 1))
 
         def chunk_sum(name, t, c):
             c0, c1 = CHUNKS[c]
             if name == "p":
                 pre[t, c] = work.tile([P, c1 - c0], F32, name="pre", bufs=4, align_bytes=64)
-                nc.vector.tensor_tensor(out=pre[t, c][:], in0=banks[t, c][0], in1=bias_all[:, c0:c1], op=ALU.add)
+                if c < 3:
+                    copy_on(P_ENGINE[c], pre[t, c][:], banks[t, c][0])
+                else:
+                    nc.vector.tensor_tensor(out=pre[t, c][:], in0=banks[t, c][0], in1=bias_all[:], op=ALU.add)
             else:
                 nc.vector.tensor_tensor(out=pre[t, c][:], in0=banks[t, c][1], in1=pre[t, c][:], op=ALU.add)
 
@@ -346,7 +360,7 @@ def tile_share_lstm_cell_pa_kernel(
         def weight_transposes(tag, wt, e, block, count, engine):
             ps = psum.tile([P, count, P], BF16, name="wt_ps", tag=tag, bufs=(3 if tag == "rot" else 1))
             for j in range(count):
-                nc.tensor.matmul(ps[:, j, :], lhsT=block(j)[:, e :: 2], rhs=ident_b[:], start=True, stop=True)
+                nc.tensor.matmul(ps[:, j, :], lhsT=block(j), rhs=ident_b[:], start=True, stop=True)
             copy_on(engine, wt[:, e, :], ps[:].rearrange("p j n -> p (j n)"))
 
         def x_transposes(t):
@@ -357,7 +371,7 @@ def tile_share_lstm_cell_pa_kernel(
             c0, c1 = CHUNKS[c]
             ps = psum.tile([P, c1 - c0], F32, name="bias_ps", tag="rot", bufs=3)
             nc.tensor.matmul(ps[:], lhsT=ones[:], rhs=bias_rows[:, c0:c1], start=True, stop=True)
-            nc.scalar.copy(out=bias_all[:, c0:c1], in_=ps[:])
+            nc.scalar.copy(out=bias_all[:], in_=ps[:])
 
         def bias_columns():
             ps = psum.tile([P, NG // P, 2], F32, name="bias_col_ps", tag="rot", bufs=3)
@@ -379,12 +393,10 @@ def tile_share_lstm_cell_pa_kernel(
         x_transposes(0)
         x_copy(0, "dve")
         quantize(0)
-        weight_transposes("gA", wt_hh, 0, lambda j: whh_raw[:, j, :], HH_BLOCKS, "act")
+        weight_transposes("gA", wt_hh, 0, lambda j: whh_raw[:, j, :P], HH_BLOCKS, "act")
         hs_transposes(0, 0, 1)
         hs_copy(0, "dve", 0, 1)
-        weight_transposes("gB", wt_hh, 1, lambda j: whh_raw[:, j, :], HH_BLOCKS, "dve")
-        bias_broadcast(0)
-        bias_broadcast(1)
+        weight_transposes("gB", wt_hh, 1, lambda j: whh_raw[:, j, P:], HH_BLOCKS, "dve")
         x_sort(1)
         x_sort(2)
 
@@ -405,9 +417,8 @@ def tile_share_lstm_cell_pa_kernel(
         quantize(1)
         for m, factor in ((m1, 1.0), (m2, 0.5), (m3, 1.0 / 3.0)):
             nc.vector.tensor_scalar(out=m[:], in0=mask_sb[:], scalar1=factor, scalar2=None, op0=ALU.mult)
-        weight_transposes("sX", wt_s, 0, wsh_block, 6, "act")
-        weight_transposes("sP", wt_s, 1, wsh_block, 6, "dve")
-        bias_broadcast(2)
+        weight_transposes("sX", wt_s, 0, lambda j: wsh_block(j)[:, 0::2], 6, "act")
+        weight_transposes("sP", wt_s, 1, lambda j: wsh_block(j)[:, 1::2], 6, "dve")
         bias_columns()
         steps(("fc", "ig"), 0)
         x_sort(3)
@@ -490,8 +501,8 @@ def tile_share_lstm_cell_pa_kernel(
             mx_copy(UNITS[-1], PAIRS[n], "act")
         for q in range(4):
             gate_round(t, q, nothing)
-        steps(("d0", "d1", "hs0", "d2", "e1", "f2", "s1"), r)
-        store(r, (1, 2, 3))
+        steps(("d0", "d1", "hs0", "d2"), r)
+        store(r, (1, 2))
         gates[t] = work.tile([P, NG], F32, name="gates", bufs=3, align_bytes=64)
         nc.scalar.activation(out=gate(t, 1), in_=banks[t, "gB"][:, :DH], func=ACT.Sigmoid)
         nc.scalar.activation(out=gate(t, 0), in_=banks[t, "gA"][:, :DH], func=ACT.Sigmoid)
@@ -502,17 +513,16 @@ def tile_share_lstm_cell_pa_kernel(
         for q in range(2):
             gate_round(t, 5 + q, nothing)
         act_o(t)
-        step("fc", t)
-        step("e2", r)
-        step("ig", t)
-        step("s2", r)
-        store(r, (4,))
-        step("ct", t)
-        store(t, (0,))
-        act_tanh_c(t)
         for n, tag in ((5, "sX"), (6, "sP")):
             nc.scalar.activation(out=gate(t, n), in_=banks[t, tag][:, :DH], func=ACT.Sigmoid)
-        steps(("d0", "s0", "d1", "d2", "e1", "f2", "s1"), t)
+        for mine, earlier in (("fc", "e1"), ("ig", "f2"), ("ct", "s1"), ("d0", "e2"), ("d1", "s2")):
+            step(mine, t)
+            if mine == "ct":
+                store(t, (0,))
+                act_tanh_c(t)
+            step(earlier, r)
+        store(r, (3, 4))
+        steps(("s0", "d2", "e1", "f2", "s1"), t)
         store(t, (2, 3))
         steps(("h", "e2"), t)
         store(t, (1,))

@@ -19,16 +19,29 @@ ALU = mybir.AluOpType
 
 P = 128
 TILES = B // P
+LAST = TILES - 1
 PASSES = DI // 512
+BLOCKS = NG // P
 HH_BLOCKS = 4 * DH // P
+TURNED_BLOCKS = 10
+TURNED_COLS = TURNED_BLOCKS * P
+DIRECT_COLS = NG - TURNED_COLS
+CHUNKS = [(0, 2 * DH), (2 * DH, 4 * DH), (4 * DH, TURNED_COLS), (TURNED_COLS, NG)]
+B12 = 3
 PAIRS = [(0, 2), (1, 3), (6, 8), (7, 9), (4, 5), (10, 12), (11, 13)]
-P_ENGINE = ("act", "dve", "act")
-UNITS = [(0, 1), (1, 2), (3, 2), (5, 2), (7, 1)]
-T_BLOCKS = 10
-T_COLS = T_BLOCKS * P
-A_COLS = NG - T_COLS
-CHUNKS = [(0, 512), (512, 1024), (1024, T_COLS), (T_COLS, NG)]
-SH = 3 * DH
+O_PAIR = 4
+B12_PAIRS = (5, 6)
+BATCHES = [(0, 1), (1, 2), (3, 2), (5, 2), (7, 1)]
+X_AHEAD = 3
+EARLY = 2
+
+ROT_BANKS = 3
+MX_BUFS = 12
+PRE_BUFS = 4
+DEEP = 3
+
+G_I, G_F, G_G, G_O, G_B0, G_B1, G_B2 = range(7)
+O_CT, O_H, O_S0, O_S1, O_S2 = range(5)
 
 
 def tile_share_lstm_cell_pa_kernel(
@@ -43,31 +56,39 @@ def tile_share_lstm_cell_pa_kernel(
         psum = ctx.enter_context(tc.psum_pool(name="psum", bufs=1))
         ctx.enter_context(tc.manual_schedule())
 
-        def rows(ap):
+        def by_tile(ap):
             return ap.rearrange("(p t) d -> p t d", t=TILES)
+
+        def as_row(vec):
+            return vec.rearrange("(a n) -> a n", a=1)
 
         x_sb, state_sb = {}, {}
 
-        def load_x(t0, n):
-            xt = keep.tile([P, n, DI], BF16, name="x%d" % t0, align_bytes=64)
-            nc.sync.dma_start(out=xt[:], in_=rows(x)[:, t0 : t0 + n, :])
-            for i in range(n):
+        def load_x(t0, count):
+            xt = keep.tile([P, count, DI], BF16, name="x%d" % t0, align_bytes=64)
+            nc.sync.dma_start(out=xt[:], in_=by_tile(x)[:, t0 : t0 + count, :])
+            for i in range(count):
                 x_sb[t0 + i] = xt[:, i, :]
 
-        def load_state(key, src, t0, n):
-            st = keep.tile([P, n, DH], BF16, name="%s%d" % (key, t0), align_bytes=64)
-            nc.sync.dma_start(out=st[:], in_=rows(src)[:, t0 : t0 + n, :])
-            for i in range(n):
+        def load_state(key, src, t0, count):
+            st = keep.tile([P, count, DH], BF16, name="%s%d" % (key, t0), align_bytes=64)
+            nc.sync.dma_start(out=st[:], in_=by_tile(src)[:, t0 : t0 + count, :])
+            for i in range(count):
                 state_sb[key, t0 + i] = st[:, i, :]
 
-        def load_words(name, c0, c1):
+        def load_w_codes(name, c0, c1):
             wt = keep.tile([P, PASSES, 2 * (c1 - c0)], U8, name=name, align_bytes=64)
             src = weight_ih_words.rearrange("g p n -> p g n")[:, :, 2 * c0 : 2 * c1]
             nc.sync.dma_start(out=wt[:].bitcast(I32), in_=src.bitcast(I32))
             return wt
 
-        plane = keep.tile([P, PASSES, NG], U8, name="plane", align_bytes=64)
-        nc.vector.memset(plane[:].bitcast(I32), 0)
+        def load_plain_weight(name, w):
+            wr = keep.tile([P, w.shape[0] // P, DH], BF16, name=name, align_bytes=64)
+            nc.sync.dma_start(out=wr[:], in_=w.rearrange("(j p) k -> p j k", p=P))
+            return wr
+
+        w_scales = keep.tile([P, PASSES, NG], U8, name="w_scales", align_bytes=64)
+        nc.vector.memset(w_scales[:].bitcast(I32), 0)
 
         bias_rows = keep.tile([P, NG], BF16, name="bias_rows", align_bytes=64)
         ones = keep.tile([P, P], BF16, name="ones", align_bytes=64)
@@ -80,451 +101,441 @@ def tile_share_lstm_cell_pa_kernel(
         nc.vector.tensor_copy(out=ident_b[:], in_=ident_f[:])
 
         states = (("h", h_minors), ("s0", s0), ("s1", s1), ("s2", s2))
-        load_x(0, 1)
-        whh_raw = keep.tile([P, HH_BLOCKS, DH], BF16, name="whh_raw", align_bytes=64)
-        nc.sync.dma_start(out=whh_raw[:], in_=weight_hh.rearrange("(j p) k -> p j k", p=P))
-        load_state("h", h_minors, 0, 2)
-        words_hh = load_words("words_hh", 0, T_COLS)
+        load_x(*BATCHES[0])
+        whh_raw = load_plain_weight("whh_raw", weight_hh)
+        load_state(*states[0], 0, EARLY)
+        w_codes_lo = load_w_codes("w_codes_lo", 0, TURNED_COLS)
         for q in range(4):
             nc.sync.dma_start(
-                out=plane[32 * q : 32 * q + 4, :, :].bitcast(I32),
+                out=w_scales[32 * q : 32 * q + 4, :, :].bitcast(I32),
                 in_=weight_ih_scales[:, 4 * q : 4 * q + 4, :].rearrange("g r n -> r g n").bitcast(I32),
             )
-        nc.sync.dma_start(out=bias_rows[0:1, :], in_=bias_ih.rearrange("(a n) -> a n", a=1))
-        nc.sync.dma_start(out=bias_rows[1:2, : 4 * DH], in_=bias_hh.rearrange("(a n) -> a n", a=1))
-        load_x(1, 2)
+        nc.sync.dma_start(out=bias_rows[0:1, :], in_=as_row(bias_ih))
+        nc.sync.dma_start(out=bias_rows[1:2, : 4 * DH], in_=as_row(bias_hh))
+        load_x(*BATCHES[1])
         for i, vec in enumerate((bias_sh0, bias_sh1, bias_sh2)):
-            nc.sync.dma_start(out=bias_rows[1:2, DH * (4 + i) : DH * (5 + i)], in_=vec.rearrange("(a n) -> a n", a=1))
+            nc.sync.dma_start(out=bias_rows[1:2, DH * (4 + i) : DH * (5 + i)], in_=as_row(vec))
         for key, src in states[1:]:
-            load_state(key, src, 0, 2)
-        wsh_raw = []
-        for i, w in enumerate((weight_sh0, weight_sh1, weight_sh2)):
-            wr = keep.tile([P, 2, DH], BF16, name="wsh_raw%d" % i, align_bytes=64)
-            nc.sync.dma_start(out=wr[:], in_=w.rearrange("(j p) k -> p j k", p=P))
-            wsh_raw.append(wr)
+            load_state(key, src, 0, EARLY)
+        wsh_raw = [load_plain_weight("wsh_raw%d" % i, w) for i, w in enumerate((weight_sh0, weight_sh1, weight_sh2))]
         nc.sync.dma_start(out=mask_sb[:], in_=mask.rearrange("(p t) -> p t", t=TILES))
-        load_state("c", c_minors, 0, 2)
-        words_s = load_words("words_s", T_COLS, NG)
-        load_x(3, 2)
+        load_state("c", c_minors, 0, EARLY)
+        w_codes_hi = load_w_codes("w_codes_hi", TURNED_COLS, NG)
+        load_x(*BATCHES[2])
         for key, src in states:
-            load_state(key, src, 2, TILES - 2)
-        load_state("c", c_minors, 2, TILES - 2)
-        load_x(5, 3)
+            load_state(key, src, EARLY, TILES - EARLY)
+        load_state("c", c_minors, EARLY, TILES - EARLY)
+        load_x(BATCHES[3][0], TILES - BATCHES[3][0])
 
         wt_hh = keep.tile([P, 2, 4 * DH], BF16, name="wt_hh", align_bytes=64)
-        wt_s = keep.tile([P, 2, 3 * DH], BF16, name="wt_s", align_bytes=64)
-        bias_hh_col = keep.tile([P, NG // P], F32, name="bias_hh_col")
-        bias_all = keep.tile([P, A_COLS], F32, name="bias_all", align_bytes=64)
-        m1 = keep.tile([P, TILES], F32, name="m1")
-        m2 = keep.tile([P, TILES], F32, name="m2")
-        m3 = keep.tile([P, TILES], F32, name="m3")
+        wt_sh = keep.tile([P, 2, 3 * DH], BF16, name="wt_sh", align_bytes=64)
+        bias_col = keep.tile([P, BLOCKS], F32, name="bias_col")
+        bias_b12 = keep.tile([P, DIRECT_COLS], F32, name="bias_b12", align_bytes=64)
+        mask_1 = keep.tile([P, TILES], F32, name="mask_1")
+        mask_half = keep.tile([P, TILES], F32, name="mask_half")
+        mask_third = keep.tile([P, TILES], F32, name="mask_third")
 
-        grouped, codes, scales, mx_sb, hs_t, gates, tanh_c, outs, banks = {}, {}, {}, {}, {}, {}, {}, {}, {}
-        xt_ps, hs_ps, mx_ps, pre, x_sorted = {}, {}, {}, {}, {}
+        x_sorted, x_ps, x_grouped, x_codes, x_scales = {}, {}, {}, {}, {}
+        states_ps, states_t, pair_ps, mx_turned = {}, {}, {}, {}
+        banks, chunk_ps, pre, gates, tanh_c, outs = {}, {}, {}, {}, {}, {}
 
         def copy_on(engine, out, in_):
-            if engine == "act":
+            if engine == "scalar":
                 nc.scalar.copy(out=out, in_=in_)
             else:
                 nc.vector.tensor_copy(out=out, in_=in_)
 
+        def batch_of(t):
+            batch = BATCHES[(t + 1) // 2]
+            return batch, t - batch[0]
+
+        def nothing():
+            return None
+
         def x_sort(t):
-            x_sorted[t] = work.tile([P, PASSES, 2, P], F32, name="x_sorted", bufs=3, align_bytes=64)
+            x_sorted[t] = work.tile([P, PASSES, 2, P], F32, name="x_sorted", bufs=DEEP, align_bytes=64)
             words = x_sb[t].bitcast(F32).rearrange("r (g p u) -> r g u p", g=PASSES, u=2)
             nc.vector.tensor_copy(out=x_sorted[t][:], in_=words)
 
-        def x_transpose(t, i):
-            g, u = divmod(i, 2)
-            if i == 0:
-                xt_ps[t] = psum.tile([P, PASSES, 2, P], F32, name="xt_ps", tag="rot", bufs=3)
-            nc.tensor.transpose(xt_ps[t][:, g, u, :], x_sorted[t][:, g, u, :], ident_f[:])
+        def x_turn(t, engine):
+            x_transposes(t)
+            x_copy(t, engine)
 
-        def unit_of(t):
-            unit = UNITS[(t + 1) // 2]
-            return unit, t - unit[0]
+        def x_transposes(t):
+            x_ps[t] = psum.tile([P, PASSES, 2, P], F32, name="x_ps", tag="rot", bufs=ROT_BANKS)
+            for g in range(PASSES):
+                for u in range(2):
+                    nc.tensor.transpose(x_ps[t][:, g, u, :], x_sorted[t][:, g, u, :], ident_f[:])
 
         def x_copy(t, engine):
-            unit, tt = unit_of(t)
-            if tt == 0:
-                grouped[unit] = work.tile([P, PASSES, unit[1], P, 2], F32, name="grouped", align_bytes=64)
-            copy_on(engine, grouped[unit][:, :, tt, :, :], xt_ps[t][:].rearrange("p g u r -> p g r u"))
+            batch, place = batch_of(t)
+            if place == 0:
+                x_grouped[batch] = work.tile([P, PASSES, batch[1], P, 2], F32, name="x_grouped", align_bytes=64)
+            copy_on(engine, x_grouped[batch][:, :, place, :, :], x_ps[t][:].rearrange("p g u r -> p g r u"))
 
-        def quantize(t):
-            unit = unit_of(t)[0]
-            codes[unit] = work.tile([P, PASSES, unit[1] * P], U32, name="codes", bufs=3, align_bytes=64)
-            scales[unit] = work.tile([P, PASSES, unit[1] * P], U8, name="scales", bufs=3, align_bytes=64)
+        def quantize(batch):
+            x_codes[batch] = work.tile([P, PASSES, batch[1] * P], U32, name="x_codes", bufs=DEEP, align_bytes=64)
+            x_scales[batch] = work.tile([P, PASSES, batch[1] * P], U8, name="x_scales", bufs=DEEP, align_bytes=64)
             nc.vector.quantize_mx(
-                out=codes[unit][:].rearrange("p g c -> p (g c)").bitcast(E5M2X4),
-                scales=scales[unit][:].rearrange("p g c -> p (g c)"),
-                in_=grouped[unit][:].rearrange("p g t r u -> p (g t r u)").bitcast(BF16),
+                out=x_codes[batch][:].rearrange("p g c -> p (g c)").bitcast(E5M2X4),
+                scales=x_scales[batch][:].rearrange("p g c -> p (g c)"),
+                in_=x_grouped[batch][:].rearrange("p g t r u -> p (g t r u)").bitcast(BF16),
             )
 
-        def hs_transposes(t, first=0, last=4):
-            hs_ps[t] = psum.tile([P, 4, P], F32, name="hs_ps", tag="rot", bufs=3)
+        def states_turn(t, engine, first=0, last=4):
+            states_ps[t] = psum.tile([P, 4, P], F32, name="states_ps", tag="rot", bufs=ROT_BANKS)
             for i in range(first, last):
                 src = state_sb[states[i][0], t]
                 if i == 0:
                     for e in range(2):
                         cols = slice(P * e, P * (e + 1))
-                        nc.tensor.transpose(hs_ps[t][:, i, :].bitcast(BF16)[:, cols], src[:, cols], ident_b[:])
+                        nc.tensor.transpose(states_ps[t][:, i, :].bitcast(BF16)[:, cols], src[:, cols], ident_b[:])
                 else:
-                    nc.tensor.transpose(hs_ps[t][:, i, :], src.bitcast(F32), ident_f[:])
-
-        def hs_copy(t, engine, first=0, last=4):
+                    nc.tensor.transpose(states_ps[t][:, i, :], src.bitcast(F32), ident_f[:])
             if first == 0:
-                hs_t[t] = work.tile([P, 4, P], F32, name="hs_t", align_bytes=64)
-            copy_on(engine, hs_t[t][:, first:last, :], hs_ps[t][:, first:last, :])
+                states_t[t] = work.tile([P, 4, P], F32, name="states_t", align_bytes=64)
+            copy_on(engine, states_t[t][:, first:last, :], states_ps[t][:, first:last, :])
 
         def state_t(t, i, e):
-            values = hs_t[t][:, i, :].bitcast(BF16)
-            return values[:, P * e : P * (e + 1)] if i == 0 else values[:, e :: 2]
+            values = states_t[t][:, i, :].bitcast(BF16)
+            return values[:, P * e : P * (e + 1)] if i == 0 else values[:, e::2]
 
-        def mx_pair(s, pair):
-            ps = psum.tile([P, 2, s[1] * P], F32, name="mx_ps", tag="rot", bufs=3)
-            mx_ps[s, pair] = ps
-            for i, j in enumerate(pair):
-                words, jj = (words_hh, j) if j < T_BLOCKS else (words_s, j - T_BLOCKS)
+        def weight_turn(bank, wt, e, blocks, engine):
+            ps = psum.tile([P, len(blocks), P], BF16, name="weight_ps", tag=bank)
+            for j, block in enumerate(blocks):
+                nc.tensor.matmul(ps[:, j, :], lhsT=block, rhs=ident_b[:], start=True, stop=True)
+            copy_on(engine, wt[:, e, :], ps[:].rearrange("p j n -> p (j n)"))
+
+        def whh_blocks(e):
+            return [whh_raw[:, j, P * e : P * (e + 1)] for j in range(HH_BLOCKS)]
+
+        def wsh_blocks(e):
+            return [wr[:, j, e::2] for wr in wsh_raw for j in range(2)]
+
+        def bias_setup():
+            ps = psum.tile([P, BLOCKS], F32, name="bias_col_ps", tag="rot", bufs=ROT_BANKS)
+            for j in range(BLOCKS):
+                nc.tensor.matmul(ps[:, j : j + 1], lhsT=bias_rows[:, P * j : P * (j + 1)], rhs=ones[:, 0:1],
+                                 start=True, stop=True)
+            nc.scalar.copy(out=bias_col[:], in_=ps[:])
+            ps = psum.tile([P, DIRECT_COLS], F32, name="bias_b12_ps", tag="rot", bufs=ROT_BANKS)
+            nc.tensor.matmul(ps[:], lhsT=ones[:], rhs=bias_rows[:, TURNED_COLS:], start=True, stop=True)
+            nc.scalar.copy(out=bias_b12[:], in_=ps[:])
+
+        def w_codes(g, c0, c1):
+            tile, first = (w_codes_lo, 0) if c1 <= TURNED_COLS else (w_codes_hi, TURNED_COLS)
+            return tile[:, g, 2 * (c0 - first) : 2 * (c1 - first)].bitcast(E2M1X4)
+
+        def pair_mx(batch, n):
+            ps = psum.tile([P, 2, batch[1] * P], F32, name="pair_ps", tag="rot", bufs=ROT_BANKS)
+            pair_ps[batch, n] = ps
+            for i, j in enumerate(PAIRS[n]):
                 for g in range(PASSES):
                     nc.tensor.matmul_mx(
                         out=ps[:, i, :],
-                        lhsT=words[:, g, 2 * P * jj : 2 * P * (jj + 1)].bitcast(E2M1X4),
-                        lhsT_scale=plane[:, g, P * j : P * (j + 1)],
-                        rhs=codes[s][:, g, :].bitcast(E5M2X4),
-                        rhs_scale=scales[s][:, g, :],
+                        lhsT=w_codes(g, P * j, P * (j + 1)),
+                        lhsT_scale=w_scales[:, g, P * j : P * (j + 1)],
+                        rhs=x_codes[batch][:, g, :].bitcast(E5M2X4),
+                        rhs_scale=x_scales[batch][:, g, :],
                         start=(g == 0),
                         stop=(g == PASSES - 1),
                     )
 
-        def mx_copy(s, pair, engine):
-            sb = work.tile([P, 2, s[1] * P], F32, name="mx_sb", bufs=12, align_bytes=64)
-            ps = mx_ps[s, pair]
-            j0, j1 = pair
-            for i, j in enumerate(pair):
-                mx_sb[s, j] = sb[:, i, :]
-            if engine == "act":
-                for i, j in enumerate(pair):
-                    nc.scalar.activation(out=sb[:, i, :], in_=ps[:, i, :], func=ACT.Identity, bias=bias_hh_col[:, j : j + 1])
+        def pair_copy(batch, n, engine="scalar"):
+            sb = work.tile([P, 2, batch[1] * P], F32, name="mx_turned", bufs=MX_BUFS, align_bytes=64)
+            ps = pair_ps[batch, n]
+            j0, j1 = PAIRS[n]
+            mx_turned[batch, j0], mx_turned[batch, j1] = sb[:, 0, :], sb[:, 1, :]
+            if engine == "scalar":
+                for i, j in enumerate(PAIRS[n]):
+                    nc.scalar.activation(out=sb[:, i, :], in_=ps[:, i, :], func=ACT.Identity, bias=bias_col[:, j : j + 1])
             else:
-                both = bias_hh_col[:, j0 : j1 + 1 : j1 - j0].unsqueeze(2).to_broadcast([P, 2, s[1] * P])
+                both = bias_col[:, j0 : j1 + 1 : j1 - j0].unsqueeze(2).to_broadcast([P, 2, batch[1] * P])
                 nc.vector.tensor_tensor(out=sb[:], in0=ps[:], in1=both, op=ALU.add)
 
-        def open_group(t, j, tag, q):
-            s, tt = unit_of(t)
+        def open_group(t, j, bank, q):
+            batch, place = batch_of(t)
             if q == 0:
-                banks[t, tag] = psum.tile([P, 4 * P], F32, name=tag, tag=tag)
-            nc.tensor.matmul(banks[t, tag][:, P * q : P * (q + 1)], lhsT=mx_sb[s, j][:, P * tt : P * (tt + 1)],
-                             rhs=ident_f[:], is_transpose=True, start=True, stop=False)
+                banks[t, bank] = psum.tile([P, 4 * P], F32, name=bank, tag=bank)
+            nc.tensor.matmul(banks[t, bank][:, P * q : P * (q + 1)],
+                             lhsT=mx_turned[batch, j][:, P * place : P * (place + 1)], rhs=ident_f[:],
+                             is_transpose=True, start=True, stop=False)
 
-        def plain_pass(t, j, tag, q, e):
-            state, wt, jj = (0, wt_hh, j) if j < HH_BLOCKS else (j // 2 - 3, wt_s, j - HH_BLOCKS)
-            nc.tensor.matmul(banks[t, tag][:, P * q : P * (q + 1)], lhsT=state_t(t, state, e),
-                             rhs=wt[:, e, P * jj : P * (jj + 1)], start=False, stop=(e == 1))
+        def plain_pass(t, j, bank, q, e):
+            if j < HH_BLOCKS:
+                state, weight = 0, wt_hh[:, e, P * j : P * (j + 1)]
+            else:
+                jj = j - HH_BLOCKS
+                state, weight = 1 + jj // 2, wt_sh[:, e, P * jj : P * (jj + 1)]
+            nc.tensor.matmul(banks[t, bank][:, P * q : P * (q + 1)], lhsT=state_t(t, state, e), rhs=weight,
+                             start=False, stop=(e == 1))
 
-        def gate_round(t, n, between):
-            q, tags = (n, ("gA", "gB")) if n < 4 else (n - 5, ("sX", "sP"))
-            blocks = list(zip(PAIRS[n], tags))
-            for j, tag in blocks:
-                open_group(t, j, tag, q)
+        def pair_groups(t, n, between):
+            q, pair_banks = (n, "AB") if n < O_PAIR else (n - B12_PAIRS[0], "DE")
+            blocks = list(zip(PAIRS[n], pair_banks))
+            for j, bank in blocks:
+                open_group(t, j, bank, q)
             for e in range(2):
-                for j, tag in blocks:
-                    plain_pass(t, j, tag, q, e)
+                for j, bank in blocks:
+                    plain_pass(t, j, bank, q, e)
                 if e == 0:
                     between()
 
-        def o_group(t, q):
-            j = PAIRS[4][q]
-            open_group(t, j, "gC", q)
-            for e in range(2):
-                plain_pass(t, j, "gC", q, e)
+        def o_groups(t):
+            for q, j in enumerate(PAIRS[O_PAIR]):
+                open_group(t, j, "C", q)
+                for e in range(2):
+                    plain_pass(t, j, "C", q, e)
 
-        def chunk_products(t, c, tags, between):
-            unit, tt = unit_of(t)
+        def chunk_products(t, c, chunk_banks, between):
+            batch, place = batch_of(t)
             c0, c1 = CHUNKS[c]
-            if len(tags) == 2:
-                mx_out = psum.tile([P, c1 - c0], F32, name="mx_out", tag=tags[0])[:]
-                plain_out = psum.tile([P, c1 - c0], F32, name="plain_out", tag=tags[1])[:]
+            if len(chunk_banks) == 2:
+                mx_out = psum.tile([P, c1 - c0], F32, name="mx_out", tag=chunk_banks[0])[:]
+                plain_out = psum.tile([P, c1 - c0], F32, name="plain_out", tag=chunk_banks[1])[:]
             else:
-                both = psum.tile([P, 2, c1 - c0], F32, name="both_out", tag=tags[0])
-                mx_out, plain_out = both[:, 0, :], both[:, 1, :]
-            banks[t, c] = (mx_out, plain_out)
-            words, w0 = (words_hh, 0) if c1 <= T_COLS else (words_s, T_COLS)
+                halves = psum.tile([P, 2, c1 - c0], F32, name="halves", tag=chunk_banks)
+                mx_out, plain_out = halves[:, 0, :], halves[:, 1, :]
+            chunk_ps[t, c] = (mx_out, plain_out)
+            rows = slice(P * place, P * (place + 1))
             for g in range(PASSES):
                 nc.tensor.matmul_mx(
                     out=mx_out,
-                    lhsT=codes[unit][:, g, P * tt : P * (tt + 1)].bitcast(E5M2X4),
-                    lhsT_scale=scales[unit][:, g, P * tt : P * (tt + 1)],
-                    rhs=words[:, g, 2 * (c0 - w0) : 2 * (c1 - w0)].bitcast(E2M1X4),
-                    rhs_scale=plane[:, g, c0:c1],
+                    lhsT=x_codes[batch][:, g, rows].bitcast(E5M2X4),
+                    lhsT_scale=x_scales[batch][:, g, rows],
+                    rhs=w_codes(g, c0, c1),
+                    rhs_scale=w_scales[:, g, c0:c1],
                     start=(g == 0),
                     stop=(g == PASSES - 1),
                 )
             between()
-            if c1 <= 4 * DH:
-                parts = [(0, wt_hh, c0, c1, 0)]
+            if c == B12:
+                for n in range(2):
+                    for e in range(2):
+                        nc.tensor.matmul(plain_out[:, DH * n : DH * (n + 1)], lhsT=state_t(t, 2 + n, e),
+                                         rhs=wt_sh[:, e, DH * (n + 1) : DH * (n + 2)], start=(e == 0), stop=(e == 1))
             else:
-                parts = [(n - 3, wt_s, DH * (n - 4), DH * (n - 3), DH * n - c0) for n in range(c0 // DH, c1 // DH)]
-            bias_first = c < 3
-            if bias_first:
+                state, weight = (0, wt_hh[:, :, c0:c1]) if c1 <= 4 * DH else (1, wt_sh[:, :, :DH])
                 nc.tensor.matmul(plain_out, lhsT=ones[:], rhs=bias_rows[:, c0:c1], start=True, stop=False)
-            for state, wt, w0, w1, o0 in parts:
                 for e in range(2):
-                    nc.tensor.matmul(plain_out[:, o0 : o0 + w1 - w0], lhsT=state_t(t, state, e), rhs=wt[:, e, w0:w1],
-                                     start=(e == 0 and not bias_first), stop=(e == 1))
+                    nc.tensor.matmul(plain_out, lhsT=state_t(t, state, e), rhs=weight[:, e, :], start=False, stop=(e == 1))
 
-        def chunk_sum(name, t, c):
+        def chunk_take_mx(t, c):
             c0, c1 = CHUNKS[c]
-            if name == "p":
-                pre[t, c] = work.tile([P, c1 - c0], F32, name="pre", bufs=4, align_bytes=64)
-                if c < 3:
-                    copy_on(P_ENGINE[c], pre[t, c][:], banks[t, c][0])
-                else:
-                    nc.vector.tensor_tensor(out=pre[t, c][:], in0=banks[t, c][0], in1=bias_all[:], op=ALU.add)
+            pre[t, c] = work.tile([P, c1 - c0], F32, name="pre", bufs=PRE_BUFS, align_bytes=64)
+            if c == B12:
+                nc.vector.tensor_tensor(out=pre[t, c][:], in0=chunk_ps[t, c][0], in1=bias_b12[:], op=ALU.add)
             else:
-                nc.vector.tensor_tensor(out=pre[t, c][:], in0=banks[t, c][1], in1=pre[t, c][:], op=ALU.add)
+                nc.scalar.copy(out=pre[t, c][:], in_=chunk_ps[t, c][0])
 
-        def gate(t, n, count=1):
-            return gates[t][:, DH * n : DH * (n + count)]
+        def chunk_add_plain(t, c):
+            nc.vector.tensor_tensor(out=pre[t, c][:], in0=chunk_ps[t, c][1], in1=pre[t, c][:], op=ALU.add)
 
-        def act_first(t):
-            gates[t] = work.tile([P, NG], F32, name="gates", bufs=3, align_bytes=64)
-            nc.scalar.activation(out=gate(t, 0), in_=banks[t, "gA"][:, :DH], func=ACT.Sigmoid)
-            nc.scalar.activation(out=gate(t, 2), in_=banks[t, "gA"][:, DH:], func=ACT.Tanh)
-            f_and_b0 = gates[t][:].rearrange("p (a d) -> p a d", d=DH)[:, 1:5:3, :]
-            nc.scalar.activation(out=f_and_b0, in_=banks[t, "gB"][:].rearrange("p (a d) -> p a d", d=DH), func=ACT.Sigmoid)
+        def new_gates(t):
+            gates[t] = work.tile([P, NG], F32, name="gates", bufs=DEEP, align_bytes=64)
 
-        def act_o(t):
-            nc.scalar.activation(out=gate(t, 3), in_=banks[t, "gC"][:, :DH], func=ACT.Sigmoid)
+        def gate(t, slot, count=1):
+            return gates[t][:, DH * slot : DH * (slot + count)]
 
-        def act_chunk(t, c):
-            if c == 0:
-                gates[t] = work.tile([P, NG], F32, name="gates", bufs=3, align_bytes=64)
-                nc.scalar.activation(out=gate(t, 0, 2), in_=pre[t, c][:], func=ACT.Sigmoid)
-            elif c == 1:
-                nc.scalar.activation(out=gate(t, 2), in_=pre[t, c][:, DH:], func=ACT.Tanh)
-                nc.scalar.activation(out=gate(t, 3), in_=pre[t, c][:, :DH], func=ACT.Sigmoid)
-            else:
-                nc.scalar.activation(out=gate(t, c + 2, c - 1), in_=pre[t, c][:], func=ACT.Sigmoid)
+        def sigmoid(out, in_):
+            nc.scalar.activation(out=out, in_=in_, func=ACT.Sigmoid)
 
-        def act_tanh_c(t):
+        def tanh(out, in_):
+            nc.scalar.activation(out=out, in_=in_, func=ACT.Tanh)
+
+        def half(t, bank, n):
+            return banks[t, bank][:, DH * n : DH * (n + 1)]
+
+        def tanh_of_c(t):
             tanh_c[t] = work.tile([P, DH], F32, name="tanh_c", align_bytes=64)
-            nc.scalar.activation(out=tanh_c[t][:], in_=out_slot(t, 0), func=ACT.Tanh)
+            tanh(tanh_c[t][:], out_slot(t, O_CT))
 
-        def out_slot(t, n):
-            return outs[t // 2][:, n, t % 2, :]
+        def out_slot(t, slot):
+            return outs[t // 2][:, slot, t % 2, :]
 
-        def stt(out, in0, scalar, in1, op0, op1):
+        def fused(out, in0, scalar, in1, op0, op1):
             nc.vector.scalar_tensor_tensor(out=out, in0=in0, scalar=scalar, in1=in1, op0=op0, op1=op1)
 
         def step(name, t):
             col = slice(t, t + 1)
             if name == "fc":
-                stt(gate(t, 1), gate(t, 1), m1[:, col], state_sb["c", t], ALU.mult, ALU.mult)
+                fused(gate(t, G_F), gate(t, G_F), mask_1[:, col], state_sb["c", t], ALU.mult, ALU.mult)
             elif name == "ig":
-                stt(gate(t, 0), gate(t, 0), m1[:, col], gate(t, 2), ALU.mult, ALU.mult)
+                fused(gate(t, G_I), gate(t, G_I), mask_1[:, col], gate(t, G_G), ALU.mult, ALU.mult)
             elif name == "ct":
                 if t % 2 == 0:
-                    outs[t // 2] = work.tile([P, 5, 2, DH], F32, name="outs", bufs=3, align_bytes=64)
-                nc.vector.tensor_tensor(out=out_slot(t, 0), in0=gate(t, 0), in1=gate(t, 1), op=ALU.add)
+                    outs[t // 2] = work.tile([P, 5, 2, DH], F32, name="outs", bufs=DEEP, align_bytes=64)
+                nc.vector.tensor_tensor(out=out_slot(t, O_CT), in0=gate(t, G_I), in1=gate(t, G_F), op=ALU.add)
             elif name in ("d0", "d1", "d2"):
-                n = int(name[1])
-                stt(gate(t, 4 + n), gate(t, 4 + n), float(n + 1), gate(t, 3), ALU.add, ALU.subtract)
-            elif name == "hs0":
+                n = ("d0", "d1", "d2").index(name)
+                fused(gate(t, G_B0 + n), gate(t, G_B0 + n), float(n + 1), gate(t, G_O), ALU.add, ALU.subtract)
+            elif name == "h_s0":
                 th = tanh_c[t][:].unsqueeze(1).to_broadcast([P, 2, DH])
-                stt(outs[t // 2][:, 1:3, t % 2, :], th, m1[:, col],
-                    gate(t, 3, 2).rearrange("p (a d) -> p a d", a=2), ALU.mult, ALU.mult)
+                fused(outs[t // 2][:, O_H : O_S0 + 1, t % 2, :], th, mask_1[:, col],
+                      gate(t, G_O, 2).rearrange("p (a d) -> p a d", a=2), ALU.mult, ALU.mult)
             elif name == "h":
-                stt(out_slot(t, 1), tanh_c[t][:], m1[:, col], gate(t, 3), ALU.mult, ALU.mult)
+                fused(out_slot(t, O_H), tanh_c[t][:], mask_1[:, col], gate(t, G_O), ALU.mult, ALU.mult)
             elif name == "s0":
-                stt(out_slot(t, 2), tanh_c[t][:], m1[:, col], gate(t, 4), ALU.mult, ALU.mult)
+                fused(out_slot(t, O_S0), tanh_c[t][:], mask_1[:, col], gate(t, G_B0), ALU.mult, ALU.mult)
             elif name == "e1":
-                nc.vector.tensor_tensor(out=gate(t, 5), in0=gate(t, 5), in1=out_slot(t, 2), op=ALU.subtract)
+                nc.vector.tensor_tensor(out=gate(t, G_B1), in0=gate(t, G_B1), in1=out_slot(t, O_S0), op=ALU.subtract)
             elif name == "f2":
-                stt(gate(t, 6), out_slot(t, 2), -2.0, gate(t, 6), ALU.mult, ALU.add)
+                fused(gate(t, G_B2), out_slot(t, O_S0), -2.0, gate(t, G_B2), ALU.mult, ALU.add)
             elif name == "s1":
-                stt(out_slot(t, 3), tanh_c[t][:], m2[:, col], gate(t, 5), ALU.mult, ALU.mult)
+                fused(out_slot(t, O_S1), tanh_c[t][:], mask_half[:, col], gate(t, G_B1), ALU.mult, ALU.mult)
             elif name == "e2":
-                nc.vector.tensor_tensor(out=gate(t, 6), in0=gate(t, 6), in1=out_slot(t, 3), op=ALU.subtract)
+                nc.vector.tensor_tensor(out=gate(t, G_B2), in0=gate(t, G_B2), in1=out_slot(t, O_S1), op=ALU.subtract)
             else:
-                stt(out_slot(t, 4), tanh_c[t][:], m3[:, col], gate(t, 6), ALU.mult, ALU.mult)
-
-        out_of_slot = (out_1, out_0, out_2, out_3, out_4)
-
-        def store(t, slots):
-            last_pair = t // 2 == TILES // 2 - 1
-            for n in slots:
-                if last_pair:
-                    nc.sync.dma_start(out=rows(out_of_slot[n])[:, t, :], in_=out_slot(t, n))
-                elif t % 2 == 1:
-                    nc.sync.dma_start(out=rows(out_of_slot[n])[:, t - 1 : t + 1, :], in_=outs[t // 2][:, n, :, :])
-
-        def weight_transposes(tag, wt, e, block, count, engine):
-            ps = psum.tile([P, count, P], BF16, name="wt_ps", tag=tag, bufs=(3 if tag == "rot" else 1))
-            for j in range(count):
-                nc.tensor.matmul(ps[:, j, :], lhsT=block(j), rhs=ident_b[:], start=True, stop=True)
-            copy_on(engine, wt[:, e, :], ps[:].rearrange("p j n -> p (j n)"))
-
-        def x_transposes(t):
-            for i in range(4):
-                x_transpose(t, i)
-
-        def bias_broadcast(c):
-            c0, c1 = CHUNKS[c]
-            ps = psum.tile([P, c1 - c0], F32, name="bias_ps", tag="rot", bufs=3)
-            nc.tensor.matmul(ps[:], lhsT=ones[:], rhs=bias_rows[:, c0:c1], start=True, stop=True)
-            nc.scalar.copy(out=bias_all[:], in_=ps[:])
-
-        def bias_columns():
-            ps = psum.tile([P, NG // P, 2], F32, name="bias_col_ps", tag="rot", bufs=3)
-            for j in range(NG // P):
-                nc.tensor.matmul(ps[:, j, :], lhsT=bias_rows[:, P * j : P * (j + 1)], rhs=ones[:, 0:2], start=True, stop=True)
-            nc.scalar.copy(out=bias_hh_col[:], in_=ps[:, :, 0])
-
-        def wsh_block(j):
-            return wsh_raw[j // 2][:, j % 2, :]
+                fused(out_slot(t, O_S2), tanh_c[t][:], mask_third[:, col], gate(t, G_B2), ALU.mult, ALU.mult)
 
         def steps(names, t):
             for name in names:
                 step(name, t)
 
-        def nothing():
-            return None
+        out_of_slot = (out_1, out_0, out_2, out_3, out_4)
+
+        def store(t, slots):
+            for slot in slots:
+                if t >= LAST - 1:
+                    nc.sync.dma_start(out=by_tile(out_of_slot[slot])[:, t, :], in_=out_slot(t, slot))
+                elif t % 2 == 1:
+                    nc.sync.dma_start(out=by_tile(out_of_slot[slot])[:, t - 1 : t + 1, :], in_=outs[t // 2][:, slot, :, :])
 
         x_sort(0)
-        x_transposes(0)
-        x_copy(0, "dve")
-        quantize(0)
-        weight_transposes("gA", wt_hh, 0, lambda j: whh_raw[:, j, :P], HH_BLOCKS, "act")
-        hs_transposes(0, 0, 1)
-        hs_copy(0, "dve", 0, 1)
-        weight_transposes("gB", wt_hh, 1, lambda j: whh_raw[:, j, P:], HH_BLOCKS, "dve")
+        x_turn(0, "vector")
+        quantize(BATCHES[0])
+        weight_turn("A", wt_hh, 0, whh_blocks(0), "scalar")
+        states_turn(0, "vector", 0, 1)
+        weight_turn("B", wt_hh, 1, whh_blocks(1), "vector")
         x_sort(1)
         x_sort(2)
 
-        chunk_products(0, 0, ("sX", "sP"), nothing)
-        chunk_products(0, 1, ("gA", "gB"), nothing)
-        chunk_sum("p", 0, 0)
-        chunk_sum("p", 0, 1)
-        chunk_sum("q", 0, 0)
-        chunk_sum("q", 0, 1)
-        act_chunk(0, 0)
-        x_transposes(1)
-        x_copy(1, "dve")
-        x_transposes(2)
-        x_copy(2, "act")
-        hs_transposes(0, 1, 4)
-        act_chunk(0, 1)
-        hs_copy(0, "act", 1, 4)
-        quantize(1)
-        for m, factor in ((m1, 1.0), (m2, 0.5), (m3, 1.0 / 3.0)):
-            nc.vector.tensor_scalar(out=m[:], in0=mask_sb[:], scalar1=factor, scalar2=None, op0=ALU.mult)
-        weight_transposes("sX", wt_s, 0, lambda j: wsh_block(j)[:, 0::2], 6, "act")
-        weight_transposes("sP", wt_s, 1, lambda j: wsh_block(j)[:, 1::2], 6, "dve")
-        bias_columns()
+        chunk_products(0, 0, "DE", nothing)
+        chunk_take_mx(0, 0)
+        chunk_add_plain(0, 0)
+        new_gates(0)
+        sigmoid(gate(0, G_I, 2), pre[0, 0][:])
+        x_turn(1, "vector")
+        x_turn(2, "vector")
+        chunk_products(0, 1, "AB", nothing)
+        chunk_take_mx(0, 1)
+        states_turn(0, "scalar", 1, 4)
+        quantize(BATCHES[1])
+        chunk_add_plain(0, 1)
+        weight_turn("D", wt_sh, 0, wsh_blocks(0), "scalar")
+        tanh(gate(0, G_G), pre[0, 1][:, DH:])
+        sigmoid(gate(0, G_O), pre[0, 1][:, :DH])
+        weight_turn("E", wt_sh, 1, wsh_blocks(1), "vector")
+        for scaled, factor in ((mask_1, 1.0), (mask_half, 0.5), (mask_third, 1.0 / 3.0)):
+            nc.vector.tensor_scalar(out=scaled[:], in0=mask_sb[:], scalar1=factor, scalar2=None, op0=ALU.mult)
+        bias_setup()
         steps(("fc", "ig"), 0)
-        x_sort(3)
-        chunk_products(0, 2, ("gC",), lambda: mx_pair(UNITS[1], PAIRS[0]))
-        bias_broadcast(3)
-        chunk_sum("p", 0, 2)
+        x_sort(X_AHEAD)
+        chunk_products(0, 2, "C", lambda: pair_mx(BATCHES[1], 0))
         step("ct", 0)
-        mx_copy(UNITS[1], PAIRS[0], "dve")
-        chunk_sum("q", 0, 2)
-        act_tanh_c(0)
-        hs_transposes(1)
-        hs_copy(1, "act")
-        act_chunk(0, 2)
-        chunk_products(0, 3, ("gA", "gB"), lambda: mx_pair(UNITS[1], PAIRS[1]))
-        chunk_sum("p", 0, 3)
-        mx_copy(UNITS[1], PAIRS[1], "act")
+        pair_copy(BATCHES[1], 0, "vector")
+        chunk_take_mx(0, 2)
+        tanh_of_c(0)
+        states_turn(1, "scalar")
+        chunk_products(0, B12, "AB", lambda: pair_mx(BATCHES[1], 1))
+        chunk_add_plain(0, 2)
+        sigmoid(gate(0, G_B0), pre[0, 2][:])
+        chunk_take_mx(0, B12)
+        pair_copy(BATCHES[1], 1)
         step("d0", 0)
-        chunk_sum("q", 0, 3)
-        x_transposes(3)
-        mx_pair(UNITS[1], PAIRS[2])
-        act_chunk(0, 3)
-        x_copy(3, "dve")
-        mx_copy(UNITS[1], PAIRS[2], "act")
+        chunk_add_plain(0, B12)
+        x_transposes(X_AHEAD)
+        pair_mx(BATCHES[1], 2)
+        x_copy(X_AHEAD, "vector")
+        pair_copy(BATCHES[1], 2)
+        sigmoid(gate(0, G_B1, 2), pre[0, B12][:])
 
-        for t in range(1, TILES - 1):
-            unit, follows = unit_of(t)
-            r = t - 1
-            if not follows:
-                later = {-1: [(unit, PAIRS[3])], 1: [(unit, PAIRS[4])]}
-            elif t + 2 < TILES:
-                later = {q: [(unit_of(t + 1)[0], PAIRS[n])] for n, q in enumerate((0, 2, 3))}
+        IN_CHUNK = -1
+        for t in range(1, LAST):
+            batch, place = batch_of(t)
+            prev = t - 1
+            if place == 0:
+                mx_at = {IN_CHUNK: (batch, 3), 1: (batch, O_PAIR)}
+            elif t + 1 < LAST:
+                mx_at = {q: (batch_of(t + 1)[0], n) for n, q in enumerate((0, 2, 3))}
             else:
-                later = {q: [(unit_of(t + 1)[0], PAIRS[n])] for n, q in enumerate((-1, 0, 1, 2, 3))}
+                mx_at = {q: (batch_of(t + 1)[0], n) for n, q in enumerate((IN_CHUNK, 0, 1, 2, 3))}
 
-            def pairs_at(q, later=later):
-                for a in later.get(q, []):
-                    mx_pair(*a)
+            def mx_here(q, mx_at=mx_at):
+                if q in mx_at:
+                    pair_mx(*mx_at[q])
 
-            def copies_at(q, later=later):
-                for a in later.get(q, []):
-                    mx_copy(*a, "act")
+            def copy_here(q, mx_at=mx_at):
+                if q in mx_at:
+                    pair_copy(*mx_at[q])
 
-            chunk_products(t, 3, ("sX", "sP"), lambda: pairs_at(-1))
-            copies_at(-1)
-            if t + 3 < TILES:
-                x_sort(t + 3)
-            steps(("hs0", "d1", "d2") if t == 1 else ("d0", "d1", "d2", "hs0"), r)
-            chunk_sum("p", t, 3)
-            steps(("e1", "f2", "s1"), r)
-            store(r, (1, 2, 3))
-            chunk_sum("q", t, 3)
-            step("e2", r)
-            for q in range(4):
+            chunk_products(t, B12, "DE", lambda: mx_here(IN_CHUNK))
+            copy_here(IN_CHUNK)
+            if t + X_AHEAD < TILES:
+                x_sort(t + X_AHEAD)
+            steps(("h_s0", "d1", "d2") if prev == 0 else ("d0", "d1", "d2", "h_s0"), prev)
+            chunk_take_mx(t, B12)
+            steps(("e1", "f2", "s1"), prev)
+            store(prev, (O_H, O_S0, O_S1))
+            chunk_add_plain(t, B12)
+            step("e2", prev)
+            for q in range(O_PAIR):
                 if q == 0:
-                    hs_transposes(t + 1)
-                    hs_copy(t + 1, "act")
-                if q == 2 and t + 3 < TILES:
-                    x_transposes(t + 3)
-                    x_copy(t + 3, "act")
-                gate_round(t, q, lambda: pairs_at(q))
-                if q < 3:
-                    copies_at(q)
-            if t in (1, 3, 4):
-                quantize(t + 3 - t % 2)
-            act_first(t)
-            for q in range(2):
-                o_group(t, q)
+                    states_turn(t + 1, "scalar")
+                if q == 2 and t + X_AHEAD < TILES:
+                    x_turn(t + X_AHEAD, "scalar")
+                pair_groups(t, q, lambda: mx_here(q))
+                if q < O_PAIR - 1:
+                    copy_here(q)
+            if t + X_AHEAD < TILES:
+                ahead, ahead_place = batch_of(t + X_AHEAD)
+                if ahead_place == ahead[1] - 1:
+                    quantize(ahead)
+            new_gates(t)
+            sigmoid(gate(t, G_I), half(t, "A", 0))
+            tanh(gate(t, G_G), half(t, "A", 1))
+            f_and_b0 = gates[t][:].rearrange("p (a d) -> p a d", d=DH)[:, G_F : G_B0 + 1 : G_B0 - G_F, :]
+            sigmoid(f_and_b0, banks[t, "B"][:].rearrange("p (a d) -> p a d", d=DH))
+            o_groups(t)
             steps(("ig", "fc"), t)
-            step("s2", r)
-            store(r, (4,))
+            step("s2", prev)
+            store(prev, (O_S2,))
             step("ct", t)
-            store(t, (0,))
-            act_chunk(t, 3)
-            act_o(t)
-            copies_at(3)
-            act_tanh_c(t)
-        t, r = TILES - 1, TILES - 2
-        for n in (5, 6):
-            mx_pair(UNITS[-1], PAIRS[n])
-            mx_copy(UNITS[-1], PAIRS[n], "act")
-        for q in range(4):
-            gate_round(t, q, nothing)
-        steps(("d0", "d1", "hs0", "d2"), r)
-        store(r, (1, 2))
-        gates[t] = work.tile([P, NG], F32, name="gates", bufs=3, align_bytes=64)
-        nc.scalar.activation(out=gate(t, 1), in_=banks[t, "gB"][:, :DH], func=ACT.Sigmoid)
-        nc.scalar.activation(out=gate(t, 0), in_=banks[t, "gA"][:, :DH], func=ACT.Sigmoid)
-        nc.scalar.activation(out=gate(t, 2), in_=banks[t, "gA"][:, DH:], func=ACT.Tanh)
-        nc.scalar.activation(out=gate(t, 4), in_=banks[t, "gB"][:, DH:], func=ACT.Sigmoid)
-        for q in range(2):
-            o_group(t, q)
-        for q in range(2):
-            gate_round(t, 5 + q, nothing)
-        act_o(t)
-        for n, tag in ((5, "sX"), (6, "sP")):
-            nc.scalar.activation(out=gate(t, n), in_=banks[t, tag][:, :DH], func=ACT.Sigmoid)
+            store(t, (O_CT,))
+            sigmoid(gate(t, G_B1, 2), pre[t, B12][:])
+            sigmoid(gate(t, G_O), half(t, "C", 0))
+            copy_here(O_PAIR - 1)
+            tanh_of_c(t)
+
+        prev = LAST - 1
+        for n in B12_PAIRS:
+            pair_mx(BATCHES[-1], n)
+            pair_copy(BATCHES[-1], n)
+        for q in range(O_PAIR):
+            pair_groups(LAST, q, nothing)
+        steps(("d0", "d1", "h_s0", "d2"), prev)
+        store(prev, (O_H, O_S0))
+        new_gates(LAST)
+        sigmoid(gate(LAST, G_F), half(LAST, "B", 0))
+        sigmoid(gate(LAST, G_I), half(LAST, "A", 0))
+        tanh(gate(LAST, G_G), half(LAST, "A", 1))
+        sigmoid(gate(LAST, G_B0), half(LAST, "B", 1))
+        o_groups(LAST)
+        for n in B12_PAIRS:
+            pair_groups(LAST, n, nothing)
+        sigmoid(gate(LAST, G_O), half(LAST, "C", 0))
+        sigmoid(gate(LAST, G_B1), half(LAST, "D", 0))
+        sigmoid(gate(LAST, G_B2), half(LAST, "E", 0))
         for mine, earlier in (("fc", "e1"), ("ig", "f2"), ("ct", "s1"), ("d0", "e2"), ("d1", "s2")):
-            step(mine, t)
+            step(mine, LAST)
             if mine == "ct":
-                store(t, (0,))
-                act_tanh_c(t)
-            step(earlier, r)
-        store(r, (3, 4))
-        steps(("s0", "d2", "e1", "f2", "s1"), t)
-        store(t, (2, 3))
-        steps(("h", "e2"), t)
-        store(t, (1,))
-        step("s2", t)
-        store(t, (4,))
+                store(LAST, (O_CT,))
+                tanh_of_c(LAST)
+            step(earlier, prev)
+        store(prev, (O_S1, O_S2))
+        steps(("s0", "d2", "e1", "f2", "s1"), LAST)
+        store(LAST, (O_S0, O_S1))
+        steps(("h", "e2"), LAST)
+        store(LAST, (O_H,))
+        step("s2", LAST)
+        store(LAST, (O_S2,))

from contextlib import ExitStack

import concourse.mybir as mybir
from concourse.masks import make_identity

B, DI, DH = 1024, 1024, 256
NG = 7 * DH
FLOPS = 2 * B * DI * NG + 2 * B * DH * NG

F32 = mybir.dt.float32
BF16 = mybir.dt.bfloat16
I32 = mybir.dt.int32
U32 = mybir.dt.uint32
U8 = mybir.dt.uint8
E5M2X4 = mybir.dt.float8_e5m2_x4
E2M1X4 = mybir.dt.float4_e2m1fn_x4
ACT = mybir.ActivationFunctionType
ALU = mybir.AluOpType

P = 128
TILES = B // P
LAST = TILES - 1
PASSES = DI // 512
BLOCKS = NG // P
HH_BLOCKS = 4 * DH // P
TURNED_BLOCKS = 10
TURNED_COLS = TURNED_BLOCKS * P
DIRECT_COLS = NG - TURNED_COLS
CHUNKS = [(0, 2 * DH), (2 * DH, 4 * DH), (4 * DH, TURNED_COLS), (TURNED_COLS, NG)]
B12 = 3
PAIRS = [(0, 2), (1, 3), (6, 8), (7, 9), (4, 5), (10, 12), (11, 13)]
O_PAIR = 4
B12_PAIRS = (5, 6)
BATCHES = [(0, 1), (1, 2), (3, 2), (5, 2), (7, 1)]
X_AHEAD = 3
EARLY = 2

ROT_BANKS = 3
MX_BUFS = 12
PRE_BUFS = 4
DEEP = 3

G_I, G_F, G_G, G_O, G_B0, G_B1, G_B2 = range(7)
O_CT, O_H, O_S0, O_S1, O_S2 = range(5)


def tile_share_lstm_cell_pa_kernel(
    tc, x, h_minors, c_minors, s0, s1, s2, mask, weight_ih_words, weight_ih_scales, bias_ih,
    weight_hh, bias_hh, weight_sh0, bias_sh0, weight_sh1, bias_sh1, weight_sh2, bias_sh2,
    out_0, out_1, out_2, out_3, out_4,
):
    nc = tc.nc
    with ExitStack() as ctx:
        keep = ctx.enter_context(tc.tile_pool(name="keep", bufs=1))
        work = ctx.enter_context(tc.tile_pool(name="work", bufs=2))
        psum = ctx.enter_context(tc.psum_pool(name="psum", bufs=1))
        ctx.enter_context(tc.manual_schedule())

        def by_tile(ap):
            return ap.rearrange("(p t) d -> p t d", t=TILES)

        def as_row(vec):
            return vec.rearrange("(a n) -> a n", a=1)

        x_sb, state_sb = {}, {}

        def load_x(t0, count):
            xt = keep.tile([P, count, DI], BF16, name="x%d" % t0, align_bytes=64)
            nc.sync.dma_start(out=xt[:], in_=by_tile(x)[:, t0 : t0 + count, :])
            for i in range(count):
                x_sb[t0 + i] = xt[:, i, :]

        def load_state(key, src, t0, count):
            st = keep.tile([P, count, DH], BF16, name="%s%d" % (key, t0), align_bytes=64)
            nc.sync.dma_start(out=st[:], in_=by_tile(src)[:, t0 : t0 + count, :])
            for i in range(count):
                state_sb[key, t0 + i] = st[:, i, :]

        def load_w_codes(name, c0, c1):
            wt = keep.tile([P, PASSES, 2 * (c1 - c0)], U8, name=name, align_bytes=64)
            src = weight_ih_words.rearrange("g p n -> p g n")[:, :, 2 * c0 : 2 * c1]
            nc.sync.dma_start(out=wt[:].bitcast(I32), in_=src.bitcast(I32))
            return wt

        def load_plain_weight(name, w):
            wr = keep.tile([P, w.shape[0] // P, DH], BF16, name=name, align_bytes=64)
            nc.sync.dma_start(out=wr[:], in_=w.rearrange("(j p) k -> p j k", p=P))
            return wr

        w_scales = keep.tile([P, PASSES, NG], U8, name="w_scales", align_bytes=64)
        nc.vector.memset(w_scales[:].bitcast(I32), 0)

        bias_rows = keep.tile([P, NG], BF16, name="bias_rows", align_bytes=64)
        ones = keep.tile([P, P], BF16, name="ones", align_bytes=64)
        ident_f = keep.tile([P, P], F32, name="ident_f", align_bytes=64)
        ident_b = keep.tile([P, P], BF16, name="ident_b", align_bytes=64)
        mask_sb = keep.tile([P, TILES], BF16, name="mask_sb")
        make_identity(nc, ident_f[:])
        nc.vector.memset(bias_rows[:].bitcast(I32), 0)
        nc.vector.memset(ones[:], 1.0)
        nc.vector.tensor_copy(out=ident_b[:], in_=ident_f[:])

        states = (("h", h_minors), ("s0", s0), ("s1", s1), ("s2", s2))
        load_x(*BATCHES[0])
        whh_raw = load_plain_weight("whh_raw", weight_hh)
        load_state(*states[0], 0, EARLY)
        w_codes_lo = load_w_codes("w_codes_lo", 0, TURNED_COLS)
        for q in range(4):
            nc.sync.dma_start(
                out=w_scales[32 * q : 32 * q + 4, :, :].bitcast(I32),
                in_=weight_ih_scales[:, 4 * q : 4 * q + 4, :].rearrange("g r n -> r g n").bitcast(I32),
            )
        nc.sync.dma_start(out=bias_rows[0:1, :], in_=as_row(bias_ih))
        nc.sync.dma_start(out=bias_rows[1:2, : 4 * DH], in_=as_row(bias_hh))
        load_x(*BATCHES[1])
        for i, vec in enumerate((bias_sh0, bias_sh1, bias_sh2)):
            nc.sync.dma_start(out=bias_rows[1:2, DH * (4 + i) : DH * (5 + i)], in_=as_row(vec))
        for key, src in states[1:]:
            load_state(key, src, 0, EARLY)
        wsh_raw = [load_plain_weight("wsh_raw%d" % i, w) for i, w in enumerate((weight_sh0, weight_sh1, weight_sh2))]
        nc.sync.dma_start(out=mask_sb[:], in_=mask.rearrange("(p t) -> p t", t=TILES))
        load_state("c", c_minors, 0, EARLY)
        w_codes_hi = load_w_codes("w_codes_hi", TURNED_COLS, NG)
        load_x(*BATCHES[2])
        for key, src in states:
            load_state(key, src, EARLY, TILES - EARLY)
        load_state("c", c_minors, EARLY, TILES - EARLY)
        load_x(BATCHES[3][0], TILES - BATCHES[3][0])

        wt_hh = keep.tile([P, 2, 4 * DH], BF16, name="wt_hh", align_bytes=64)
        wt_sh = keep.tile([P, 2, 3 * DH], BF16, name="wt_sh", align_bytes=64)
        bias_col = keep.tile([P, BLOCKS], F32, name="bias_col")
        bias_b12 = keep.tile([P, DIRECT_COLS], F32, name="bias_b12", align_bytes=64)
        mask_1 = keep.tile([P, TILES], F32, name="mask_1")
        mask_half = keep.tile([P, TILES], F32, name="mask_half")
        mask_third = keep.tile([P, TILES], F32, name="mask_third")

        x_sorted, x_ps, x_grouped, x_codes, x_scales = {}, {}, {}, {}, {}
        states_ps, states_t, pair_ps, mx_turned = {}, {}, {}, {}
        banks, chunk_ps, pre, gates, tanh_c, outs = {}, {}, {}, {}, {}, {}

        def copy_on(engine, out, in_):
            if engine == "scalar":
                nc.scalar.copy(out=out, in_=in_)
            else:
                nc.vector.tensor_copy(out=out, in_=in_)

        def batch_of(t):
            batch = BATCHES[(t + 1) // 2]
            return batch, t - batch[0]

        def nothing():
            return None

        def x_sort(t):
            x_sorted[t] = work.tile([P, PASSES, 2, P], F32, name="x_sorted", bufs=DEEP, align_bytes=64)
            words = x_sb[t].bitcast(F32).rearrange("r (g p u) -> r g u p", g=PASSES, u=2)
            nc.vector.tensor_copy(out=x_sorted[t][:], in_=words)

        def x_turn(t, engine):
            x_transposes(t)
            x_copy(t, engine)

        def x_transposes(t):
            x_ps[t] = psum.tile([P, PASSES, 2, P], F32, name="x_ps", tag="rot", bufs=ROT_BANKS)
            for g in range(PASSES):
                for u in range(2):
                    nc.tensor.transpose(x_ps[t][:, g, u, :], x_sorted[t][:, g, u, :], ident_f[:])

        def x_copy(t, engine):
            batch, place = batch_of(t)
            if place == 0:
                x_grouped[batch] = work.tile([P, PASSES, batch[1], P, 2], F32, name="x_grouped", align_bytes=64)
            copy_on(engine, x_grouped[batch][:, :, place, :, :], x_ps[t][:].rearrange("p g u r -> p g r u"))

        def quantize(batch):
            x_codes[batch] = work.tile([P, PASSES, batch[1] * P], U32, name="x_codes", bufs=DEEP, align_bytes=64)
            x_scales[batch] = work.tile([P, PASSES, batch[1] * P], U8, name="x_scales", bufs=DEEP, align_bytes=64)
            nc.vector.quantize_mx(
                out=x_codes[batch][:].rearrange("p g c -> p (g c)").bitcast(E5M2X4),
                scales=x_scales[batch][:].rearrange("p g c -> p (g c)"),
                in_=x_grouped[batch][:].rearrange("p g t r u -> p (g t r u)").bitcast(BF16),
            )

        def states_turn(t, engine, first=0, last=4):
            states_ps[t] = psum.tile([P, 4, P], F32, name="states_ps", tag="rot", bufs=ROT_BANKS)
            for i in range(first, last):
                src = state_sb[states[i][0], t]
                if i == 0:
                    for e in range(2):
                        cols = slice(P * e, P * (e + 1))
                        nc.tensor.transpose(states_ps[t][:, i, :].bitcast(BF16)[:, cols], src[:, cols], ident_b[:])
                else:
                    nc.tensor.transpose(states_ps[t][:, i, :], src.bitcast(F32), ident_f[:])
            if first == 0:
                states_t[t] = work.tile([P, 4, P], F32, name="states_t", align_bytes=64)
            copy_on(engine, states_t[t][:, first:last, :], states_ps[t][:, first:last, :])

        def state_t(t, i, e):
            values = states_t[t][:, i, :].bitcast(BF16)
            return values[:, P * e : P * (e + 1)] if i == 0 else values[:, e::2]

        def weight_turn(bank, wt, e, blocks, engine):
            ps = psum.tile([P, len(blocks), P], BF16, name="weight_ps", tag=bank)
            for j, block in enumerate(blocks):
                nc.tensor.matmul(ps[:, j, :], lhsT=block, rhs=ident_b[:], start=True, stop=True)
            copy_on(engine, wt[:, e, :], ps[:].rearrange("p j n -> p (j n)"))

        def whh_blocks(e):
            return [whh_raw[:, j, P * e : P * (e + 1)] for j in range(HH_BLOCKS)]

        def wsh_blocks(e):
            return [wr[:, j, e::2] for wr in wsh_raw for j in range(2)]

        def bias_setup():
            ps = psum.tile([P, BLOCKS], F32, name="bias_col_ps", tag="rot", bufs=ROT_BANKS)
            for j in range(BLOCKS):
                nc.tensor.matmul(ps[:, j : j + 1], lhsT=bias_rows[:, P * j : P * (j + 1)], rhs=ones[:, 0:1],
                                 start=True, stop=True)
            nc.scalar.copy(out=bias_col[:], in_=ps[:])
            ps = psum.tile([P, DIRECT_COLS], F32, name="bias_b12_ps", tag="rot", bufs=ROT_BANKS)
            nc.tensor.matmul(ps[:], lhsT=ones[:], rhs=bias_rows[:, TURNED_COLS:], start=True, stop=True)
            nc.scalar.copy(out=bias_b12[:], in_=ps[:])

        def w_codes(g, c0, c1):
            tile, first = (w_codes_lo, 0) if c1 <= TURNED_COLS else (w_codes_hi, TURNED_COLS)
            return tile[:, g, 2 * (c0 - first) : 2 * (c1 - first)].bitcast(E2M1X4)

        def pair_mx(batch, n):
            ps = psum.tile([P, 2, batch[1] * P], F32, name="pair_ps", tag="rot", bufs=ROT_BANKS)
            pair_ps[batch, n] = ps
            for i, j in enumerate(PAIRS[n]):
                for g in range(PASSES):
                    nc.tensor.matmul_mx(
                        out=ps[:, i, :],
                        lhsT=w_codes(g, P * j, P * (j + 1)),
                        lhsT_scale=w_scales[:, g, P * j : P * (j + 1)],
                        rhs=x_codes[batch][:, g, :].bitcast(E5M2X4),
                        rhs_scale=x_scales[batch][:, g, :],
                        start=(g == 0),
                        stop=(g == PASSES - 1),
                    )

        def pair_copy(batch, n, engine="scalar"):
            sb = work.tile([P, 2, batch[1] * P], F32, name="mx_turned", bufs=MX_BUFS, align_bytes=64)
            ps = pair_ps[batch, n]
            j0, j1 = PAIRS[n]
            mx_turned[batch, j0], mx_turned[batch, j1] = sb[:, 0, :], sb[:, 1, :]
            if engine == "scalar":
                for i, j in enumerate(PAIRS[n]):
                    nc.scalar.activation(out=sb[:, i, :], in_=ps[:, i, :], func=ACT.Identity, bias=bias_col[:, j : j + 1])
            else:
                both = bias_col[:, j0 : j1 + 1 : j1 - j0].unsqueeze(2).to_broadcast([P, 2, batch[1] * P])
                nc.vector.tensor_tensor(out=sb[:], in0=ps[:], in1=both, op=ALU.add)

        def open_group(t, j, bank, q):
            batch, place = batch_of(t)
            if q == 0:
                banks[t, bank] = psum.tile([P, 4 * P], F32, name=bank, tag=bank)
            nc.tensor.matmul(banks[t, bank][:, P * q : P * (q + 1)],
                             lhsT=mx_turned[batch, j][:, P * place : P * (place + 1)], rhs=ident_f[:],
                             is_transpose=True, start=True, stop=False)

        def plain_pass(t, j, bank, q, e):
            if j < HH_BLOCKS:
                state, weight = 0, wt_hh[:, e, P * j : P * (j + 1)]
            else:
                jj = j - HH_BLOCKS
                state, weight = 1 + jj // 2, wt_sh[:, e, P * jj : P * (jj + 1)]
            nc.tensor.matmul(banks[t, bank][:, P * q : P * (q + 1)], lhsT=state_t(t, state, e), rhs=weight,
                             start=False, stop=(e == 1))

        def pair_groups(t, n, between):
            q, pair_banks = (n, "AB") if n < O_PAIR else (n - B12_PAIRS[0], "DE")
            blocks = list(zip(PAIRS[n], pair_banks))
            for j, bank in blocks:
                open_group(t, j, bank, q)
            for e in range(2):
                for j, bank in blocks:
                    plain_pass(t, j, bank, q, e)
                if e == 0:
                    between()

        def o_groups(t):
            for q, j in enumerate(PAIRS[O_PAIR]):
                open_group(t, j, "C", q)
                for e in range(2):
                    plain_pass(t, j, "C", q, e)

        def chunk_products(t, c, chunk_banks, between):
            batch, place = batch_of(t)
            c0, c1 = CHUNKS[c]
            if len(chunk_banks) == 2:
                mx_out = psum.tile([P, c1 - c0], F32, name="mx_out", tag=chunk_banks[0])[:]
                plain_out = psum.tile([P, c1 - c0], F32, name="plain_out", tag=chunk_banks[1])[:]
            else:
                halves = psum.tile([P, 2, c1 - c0], F32, name="halves", tag=chunk_banks)
                mx_out, plain_out = halves[:, 0, :], halves[:, 1, :]
            chunk_ps[t, c] = (mx_out, plain_out)
            rows = slice(P * place, P * (place + 1))
            for g in range(PASSES):
                nc.tensor.matmul_mx(
                    out=mx_out,
                    lhsT=x_codes[batch][:, g, rows].bitcast(E5M2X4),
                    lhsT_scale=x_scales[batch][:, g, rows],
                    rhs=w_codes(g, c0, c1),
                    rhs_scale=w_scales[:, g, c0:c1],
                    start=(g == 0),
                    stop=(g == PASSES - 1),
                )
            between()
            if c == B12:
                for n in range(2):
                    for e in range(2):
                        nc.tensor.matmul(plain_out[:, DH * n : DH * (n + 1)], lhsT=state_t(t, 2 + n, e),
                                         rhs=wt_sh[:, e, DH * (n + 1) : DH * (n + 2)], start=(e == 0), stop=(e == 1))
            else:
                state, weight = (0, wt_hh[:, :, c0:c1]) if c1 <= 4 * DH else (1, wt_sh[:, :, :DH])
                nc.tensor.matmul(plain_out, lhsT=ones[:], rhs=bias_rows[:, c0:c1], start=True, stop=False)
                for e in range(2):
                    nc.tensor.matmul(plain_out, lhsT=state_t(t, state, e), rhs=weight[:, e, :], start=False, stop=(e == 1))

        def chunk_take_mx(t, c):
            c0, c1 = CHUNKS[c]
            pre[t, c] = work.tile([P, c1 - c0], F32, name="pre", bufs=PRE_BUFS, align_bytes=64)
            if c == B12:
                nc.vector.tensor_tensor(out=pre[t, c][:], in0=chunk_ps[t, c][0], in1=bias_b12[:], op=ALU.add)
            else:
                nc.scalar.copy(out=pre[t, c][:], in_=chunk_ps[t, c][0])

        def chunk_add_plain(t, c):
            nc.vector.tensor_tensor(out=pre[t, c][:], in0=chunk_ps[t, c][1], in1=pre[t, c][:], op=ALU.add)

        def new_gates(t):
            gates[t] = work.tile([P, NG], F32, name="gates", bufs=DEEP, align_bytes=64)

        def gate(t, slot, count=1):
            return gates[t][:, DH * slot : DH * (slot + count)]

        def sigmoid(out, in_):
            nc.scalar.activation(out=out, in_=in_, func=ACT.Sigmoid)

        def tanh(out, in_):
            nc.scalar.activation(out=out, in_=in_, func=ACT.Tanh)

        def half(t, bank, n):
            return banks[t, bank][:, DH * n : DH * (n + 1)]

        def tanh_of_c(t):
            tanh_c[t] = work.tile([P, DH], F32, name="tanh_c", align_bytes=64)
            tanh(tanh_c[t][:], out_slot(t, O_CT))

        def out_slot(t, slot):
            return outs[t // 2][:, slot, t % 2, :]

        def fused(out, in0, scalar, in1, op0, op1):
            nc.vector.scalar_tensor_tensor(out=out, in0=in0, scalar=scalar, in1=in1, op0=op0, op1=op1)

        def step(name, t):
            col = slice(t, t + 1)
            if name == "fc":
                fused(gate(t, G_F), gate(t, G_F), mask_1[:, col], state_sb["c", t], ALU.mult, ALU.mult)
            elif name == "ig":
                fused(gate(t, G_I), gate(t, G_I), mask_1[:, col], gate(t, G_G), ALU.mult, ALU.mult)
            elif name == "ct":
                if t % 2 == 0:
                    outs[t // 2] = work.tile([P, 5, 2, DH], F32, name="outs", bufs=DEEP, align_bytes=64)
                nc.vector.tensor_tensor(out=out_slot(t, O_CT), in0=gate(t, G_I), in1=gate(t, G_F), op=ALU.add)
            elif name in ("d0", "d1", "d2"):
                n = ("d0", "d1", "d2").index(name)
                fused(gate(t, G_B0 + n), gate(t, G_B0 + n), float(n + 1), gate(t, G_O), ALU.add, ALU.subtract)
            elif name == "h_s0":
                th = tanh_c[t][:].unsqueeze(1).to_broadcast([P, 2, DH])
                fused(outs[t // 2][:, O_H : O_S0 + 1, t % 2, :], th, mask_1[:, col],
                      gate(t, G_O, 2).rearrange("p (a d) -> p a d", a=2), ALU.mult, ALU.mult)
            elif name == "h":
                fused(out_slot(t, O_H), tanh_c[t][:], mask_1[:, col], gate(t, G_O), ALU.mult, ALU.mult)
            elif name == "s0":
                fused(out_slot(t, O_S0), tanh_c[t][:], mask_1[:, col], gate(t, G_B0), ALU.mult, ALU.mult)
            elif name == "e1":
                nc.vector.tensor_tensor(out=gate(t, G_B1), in0=gate(t, G_B1), in1=out_slot(t, O_S0), op=ALU.subtract)
            elif name == "f2":
                fused(gate(t, G_B2), out_slot(t, O_S0), -2.0, gate(t, G_B2), ALU.mult, ALU.add)
            elif name == "s1":
                fused(out_slot(t, O_S1), tanh_c[t][:], mask_half[:, col], gate(t, G_B1), ALU.mult, ALU.mult)
            elif name == "e2":
                nc.vector.tensor_tensor(out=gate(t, G_B2), in0=gate(t, G_B2), in1=out_slot(t, O_S1), op=ALU.subtract)
            else:
                fused(out_slot(t, O_S2), tanh_c[t][:], mask_third[:, col], gate(t, G_B2), ALU.mult, ALU.mult)

        def steps(names, t):
            for name in names:
                step(name, t)

        out_of_slot = (out_1, out_0, out_2, out_3, out_4)

        def store(t, slots):
            for slot in slots:
                if t >= LAST - 1:
                    nc.sync.dma_start(out=by_tile(out_of_slot[slot])[:, t, :], in_=out_slot(t, slot))
                elif t % 2 == 1:
                    nc.sync.dma_start(out=by_tile(out_of_slot[slot])[:, t - 1 : t + 1, :], in_=outs[t // 2][:, slot, :, :])

        x_sort(0)
        x_turn(0, "vector")
        quantize(BATCHES[0])
        weight_turn("A", wt_hh, 0, whh_blocks(0), "scalar")
        states_turn(0, "vector", 0, 1)
        weight_turn("B", wt_hh, 1, whh_blocks(1), "vector")
        x_sort(1)
        x_sort(2)

        chunk_products(0, 0, "DE", nothing)
        chunk_take_mx(0, 0)
        chunk_add_plain(0, 0)
        new_gates(0)
        sigmoid(gate(0, G_I, 2), pre[0, 0][:])
        x_turn(1, "vector")
        x_turn(2, "vector")
        chunk_products(0, 1, "AB", nothing)
        chunk_take_mx(0, 1)
        states_turn(0, "scalar", 1, 4)
        quantize(BATCHES[1])
        chunk_add_plain(0, 1)
        weight_turn("D", wt_sh, 0, wsh_blocks(0), "scalar")
        tanh(gate(0, G_G), pre[0, 1][:, DH:])
        sigmoid(gate(0, G_O), pre[0, 1][:, :DH])
        weight_turn("E", wt_sh, 1, wsh_blocks(1), "vector")
        for scaled, factor in ((mask_1, 1.0), (mask_half, 0.5), (mask_third, 1.0 / 3.0)):
            nc.vector.tensor_scalar(out=scaled[:], in0=mask_sb[:], scalar1=factor, scalar2=None, op0=ALU.mult)
        bias_setup()
        steps(("fc", "ig"), 0)
        x_sort(X_AHEAD)
        chunk_products(0, 2, "C", lambda: pair_mx(BATCHES[1], 0))
        step("ct", 0)
        pair_copy(BATCHES[1], 0, "vector")
        chunk_take_mx(0, 2)
        tanh_of_c(0)
        states_turn(1, "scalar")
        chunk_products(0, B12, "AB", lambda: pair_mx(BATCHES[1], 1))
        chunk_add_plain(0, 2)
        sigmoid(gate(0, G_B0), pre[0, 2][:])
        chunk_take_mx(0, B12)
        pair_copy(BATCHES[1], 1)
        step("d0", 0)
        chunk_add_plain(0, B12)
        x_transposes(X_AHEAD)
        pair_mx(BATCHES[1], 2)
        x_copy(X_AHEAD, "vector")
        pair_copy(BATCHES[1], 2)
        sigmoid(gate(0, G_B1, 2), pre[0, B12][:])

        IN_CHUNK = -1
        for t in range(1, LAST):
            batch, place = batch_of(t)
            prev = t - 1
            if place == 0:
                mx_at = {IN_CHUNK: (batch, 3), 1: (batch, O_PAIR)}
            elif t + 1 < LAST:
                mx_at = {q: (batch_of(t + 1)[0], n) for n, q in enumerate((0, 2, 3))}
            else:
                mx_at = {q: (batch_of(t + 1)[0], n) for n, q in enumerate((IN_CHUNK, 0, 1, 2, 3))}

            def mx_here(q, mx_at=mx_at):
                if q in mx_at:
                    pair_mx(*mx_at[q])

            def copy_here(q, mx_at=mx_at):
                if q in mx_at:
                    pair_copy(*mx_at[q])

            chunk_products(t, B12, "DE", lambda: mx_here(IN_CHUNK))
            copy_here(IN_CHUNK)
            if t + X_AHEAD < TILES:
                x_sort(t + X_AHEAD)
            steps(("h_s0", "d1", "d2") if prev == 0 else ("d0", "d1", "d2", "h_s0"), prev)
            chunk_take_mx(t, B12)
            steps(("e1", "f2", "s1"), prev)
            store(prev, (O_H, O_S0, O_S1))
            chunk_add_plain(t, B12)
            step("e2", prev)
            for q in range(O_PAIR):
                if q == 0:
                    states_turn(t + 1, "scalar")
                if q == 2 and t + X_AHEAD < TILES:
                    x_turn(t + X_AHEAD, "scalar")
                pair_groups(t, q, lambda: mx_here(q))
                if q < O_PAIR - 1:
                    copy_here(q)
            if t + X_AHEAD < TILES:
                ahead, ahead_place = batch_of(t + X_AHEAD)
                if ahead_place == ahead[1] - 1:
                    quantize(ahead)
            new_gates(t)
            sigmoid(gate(t, G_I), half(t, "A", 0))
            tanh(gate(t, G_G), half(t, "A", 1))
            f_and_b0 = gates[t][:].rearrange("p (a d) -> p a d", d=DH)[:, G_F : G_B0 + 1 : G_B0 - G_F, :]
            sigmoid(f_and_b0, banks[t, "B"][:].rearrange("p (a d) -> p a d", d=DH))
            o_groups(t)
            steps(("ig", "fc"), t)
            step("s2", prev)
            store(prev, (O_S2,))
            step("ct", t)
            store(t, (O_CT,))
            sigmoid(gate(t, G_B1, 2), pre[t, B12][:])
            sigmoid(gate(t, G_O), half(t, "C", 0))
            copy_here(O_PAIR - 1)
            tanh_of_c(t)

        prev = LAST - 1
        for n in B12_PAIRS:
            pair_mx(BATCHES[-1], n)
            pair_copy(BATCHES[-1], n)
        for q in range(O_PAIR):
            pair_groups(LAST, q, nothing)
        steps(("d0", "d1", "h_s0", "d2"), prev)
        store(prev, (O_H, O_S0))
        new_gates(LAST)
        sigmoid(gate(LAST, G_F), half(LAST, "B", 0))
        sigmoid(gate(LAST, G_I), half(LAST, "A", 0))
        tanh(gate(LAST, G_G), half(LAST, "A", 1))
        sigmoid(gate(LAST, G_B0), half(LAST, "B", 1))
        o_groups(LAST)
        for n in B12_PAIRS:
            pair_groups(LAST, n, nothing)
        sigmoid(gate(LAST, G_O), half(LAST, "C", 0))
        sigmoid(gate(LAST, G_B1), half(LAST, "D", 0))
        sigmoid(gate(LAST, G_B2), half(LAST, "E", 0))
        for mine, earlier in (("fc", "e1"), ("ig", "f2"), ("ct", "s1"), ("d0", "e2"), ("d1", "s2")):
            step(mine, LAST)
            if mine == "ct":
                store(LAST, (O_CT,))
                tanh_of_c(LAST)
            step(earlier, prev)
        store(prev, (O_S1, O_S2))
        steps(("s0", "d2", "e1", "f2", "s1"), LAST)
        store(LAST, (O_S0, O_S1))
        steps(("h", "e2"), LAST)
        store(LAST, (O_H,))
        step("s2", LAST)
        store(LAST, (O_S2,))
